import numpy as np
import ml_dtypes


def mxq(x, axis, fmt="e4m3"):
    dtype, down = {"e4m3": (ml_dtypes.float8_e4m3fn, 7), "e5m2": (ml_dtypes.float8_e5m2, 14)}[fmt]
    v = np.moveaxis(np.asarray(x, np.float32).astype(ml_dtypes.bfloat16).astype(np.float64), axis, -1)
    blocks = v.reshape(v.shape[:-1] + (-1, 32))
    amax = np.abs(blocks).max(-1, keepdims=True)
    byte = np.maximum(np.where(amax > 0, np.frexp(amax)[1] - 1 + 127, 0) - down, 1)
    scale = np.exp2(byte - 127.0)
    codes = (blocks / scale).astype(np.float32).astype(dtype).astype(np.float64)
    return np.moveaxis((codes * scale).reshape(v.shape), -1, axis)


WIDE = False


def mx_kscale(k):
    if not WIDE:
        return np.ones(k)
    levels = np.array([10, -10, 5, -5, 0])
    a = np.random.permutation(np.resize(levels, k // 512 * 4)).reshape(k // 512, 4)
    idx = np.arange(k)
    return np.exp2(a[idx // 512, idx % 128 // 32])


BF16 = ml_dtypes.bfloat16


def bf(x):
    return np.asarray(x, np.float32).astype(BF16)


def f64(x):
    return np.asarray(x).astype(np.float64)


S, M, L1, L2, L3, B, NG = 512, 512, 1024, 1024, 1024, 256, 4


def sigmoid(v):
    return 1.0 / (1.0 + np.exp(-v))


def lstm_cell(x, h, c, Wih, Whh, bih, bhh):
    g = (mxq(x, 1, "e4m3") @ mxq(Wih, 1, "e4m3").T) + (mxq(h, 1, "e4m3") @ mxq(Whh, 1, "e4m3").T) + (bih + bhh)
    i, f, gg, o = np.split(g, NG, axis=-1)
    c_new = sigmoid(f) * c + sigmoid(i) * np.tanh(gg)
    h_new = sigmoid(o) * np.tanh(c_new)
    return h_new, c_new


def log_softmax(v):
    shifted = v - v.max(-1, keepdims=True)
    return shifted - np.log(np.exp(shifted).sum(-1, keepdims=True))


def setup_inputs():
    rn = np.random.standard_normal
    s, t2, t3 = mx_kscale(S), mx_kscale(L2), mx_kscale(L3)
    return {
        "x": bf(rn((B, S)) * s),
        "y2": bf(rn((B, L2)) * 0.3 * t2),
        "h3": bf(rn((B, L3)) * t3), "c3": bf(rn((B, L3))),
        "Wih3": bf(rn((NG * L3, L2)) * 2.0 / np.sqrt(L2) / t2), "Whh3": bf(rn((NG * L3, L3)) * 0.7 / np.sqrt(L3) / t3),
        "bih3": bf(rn(NG * L3) * 0.3), "bhh3": bf(rn(NG * L3) * 0.3),
        "Wd": bf(rn((L3, S)) * 0.5 / np.sqrt(S) / s), "bd": bf(rn(L3) * 0.2),
        "Wm": bf(rn((M, L3)) * 3.0 / np.sqrt(L3)), "bm": bf(rn(M) * 0.5),
    }


def reference(x, y2, h3, c3, Wih3, Whh3, bih3, bhh3, Wd, bd, Wm, bm):
    y3, nc3 = lstm_cell(f64(y2), f64(h3), f64(c3), f64(Wih3), f64(Whh3), f64(bih3), f64(bhh3))
    mid = (mxq(f64(x), 1, "e4m3") @ mxq(f64(Wd), 1, "e4m3").T) + f64(bd) + y3
    motors = (mxq(mid, 1, "e4m3") @ mxq(f64(Wm), 1, "e4m3").T) + f64(bm)
    return log_softmax(motors), y3, nc3

@@ -1,0 +1,443 @@
+from contextlib import ExitStack
+
+import concourse.mybir as mybir
+from concourse.masks import make_identity
+
+F32 = mybir.dt.float32
+BF16 = mybir.dt.bfloat16
+U32 = mybir.dt.uint32
+U8 = mybir.dt.uint8
+FP8X4 = mybir.dt.float8_e4m3fn_x4
+AF = mybir.ActivationFunctionType
+ALU = mybir.AluOpType
+AX = mybir.AxisListType
+
+P = 128
+B = 256
+FLOPS = 2 * 256 * (4096 * 2048 + 1024 * 512 + 512 * 1024)
+
+EW_GPSIMD_UNTIL = 3
+MINLAG = 2
+RAW_BUFS = 8
+
+
+def tile_network_pb_kernel(
+    tc, x, y2, h3, c3, Wih3, Whh3, bih3, bhh3, Wd, bd, Wm, bm, out_0, out_1, out_2
+):
+    nc = tc.nc
+    with ExitStack() as ctx:
+        const = ctx.enter_context(tc.tile_pool(name="const", bufs=1))
+        rawp = ctx.enter_context(tc.tile_pool(name="rawp", bufs=RAW_BUFS))
+        grpp = ctx.enter_context(tc.tile_pool(name="grpp", bufs=3))
+        codp = ctx.enter_context(tc.tile_pool(name="codp", bufs=6))
+        gactp = ctx.enter_context(tc.tile_pool(name="gactp", bufs=2))
+        ew1 = ctx.enter_context(tc.tile_pool(name="ew1", bufs=1))
+        ew2 = ctx.enter_context(tc.tile_pool(name="ew2", bufs=2))
+        resp = ctx.enter_context(tc.tile_pool(name="resp", bufs=3))
+        tpp = ctx.enter_context(tc.psum_pool(name="tpp", bufs=4))
+        gtp = ctx.enter_context(tc.psum_pool(name="gtp", bufs=2))
+        otp = ctx.enter_context(tc.psum_pool(name="otp", bufs=1))
+        dpp = ctx.enter_context(tc.psum_pool(name="dpp", bufs=1))
+        ctx.enter_context(tc.manual_schedule())
+
+        braw = const.tile([P, 256], BF16)
+        bmz = const.tile([P, 512], BF16)
+        ones = const.tile([P, P], BF16)
+        dum = const.tile([P, 1], F32)
+        dum2 = const.tile([P, 1], F32)
+        nc.vector.memset(braw[:], 0.0)
+        nc.vector.memset(bmz[:], 0.0)
+        nc.vector.memset(ones[:], 1.0)
+        nc.vector.memset(dum[:], 0.0)
+        nc.scalar.dma_start(out=braw[0:16, :], in_=bih3.rearrange("(r c) -> r c", c=256))
+        nc.scalar.dma_start(out=braw[16:32, :], in_=bhh3.rearrange("(r c) -> r c", c=256))
+        nc.scalar.dma_start(out=braw[32:36, :], in_=bd.rearrange("(r c) -> r c", c=256))
+        nc.scalar.dma_start(out=bmz[0:1, :], in_=bm.rearrange("(o m) -> o m", o=1))
+        nc.scalar.activation(out=dum2[:], in_=dum[:], func=AF.Sigmoid)
+        ident = const.tile([P, P], F32)
+        make_identity(nc, ident[:])
+
+        y2raw = const.tile([P, 2, 1024], BF16)
+        h3raw = const.tile([P, 2, 1024], BF16)
+        c3raw = const.tile([P, 2, 1024], BF16)
+        xraw = const.tile([P, 2, 512], BF16)
+        wviews = [
+            w.rearrange("(g j p e) k -> j p g (e k)", g=4, j=4, p=P, e=2) for w in (Wih3, Whh3)
+        ]
+        raws = {}
+
+        def load_raw(key):
+            raw = rawp.tile([P, 4096], BF16, tag="raw", name="raw")
+            if key == "D":
+                nc.sync.dma_start(
+                    out=raw[:].rearrange("p (j f) -> p j f", j=4),
+                    in_=Wd.rearrange("(j p e) k -> p j (e k)", j=4, p=P, e=2),
+                )
+            elif key == "M":
+                nc.sync.dma_start(
+                    out=raw[:].rearrange("p (a k) -> p a k", a=4),
+                    in_=Wm.rearrange("(a p) k -> p a k", p=P),
+                )
+            else:
+                jj, gp, m = key // 4, (key % 4) // 2, key % 2
+                nc.sync.dma_start(
+                    out=raw[:].rearrange("p (g f) -> p g f", g=2),
+                    in_=wviews[m][jj][:, 2 * gp : 2 * gp + 2, :],
+                )
+            raws[key] = raw
+
+        tunits = ["A", 0, 1, 2, 3, "C", "D", 4, 5, 6, 7, 8, 9, 10, 11, "M", 12, 13, 14, 15]
+        raw_order = [u for u in tunits if u != "A" and u != "C"]
+        pos = {}
+        for i, u in enumerate(tunits):
+            pos[u] = i
+
+        nc.sync.dma_start(out=y2raw[:], in_=y2.rearrange("(t p) k -> p t k", p=P))
+        nc.sync.dma_start(out=h3raw[:], in_=h3.rearrange("(t p) k -> p t k", p=P))
+        for key in raw_order[0:4]:
+            load_raw(key)
+        nc.sync.dma_start(out=c3raw[:], in_=c3.rearrange("(t p) k -> p t k", p=P))
+        nc.sync.dma_start(out=xraw[:], in_=x.rearrange("(t p) k -> p t k", p=P))
+        for key in raw_order[4:RAW_BUFS]:
+            load_raw(key)
+        nloaded = [RAW_BUFS]
+
+        acod = const.tile([P, 1024], U32, align_bytes=64)
+        ascl = const.tile([P, 1024], U8, align_bytes=64)
+        xcod = const.tile([P, 256], U32, align_bytes=64)
+        xscl = const.tile([P, 256], U8, align_bytes=64)
+        dcod = const.tile([P, 1024], U32, align_bytes=64)
+        dscl = const.tile([P, 1024], U8, align_bytes=64)
+        wmcod = const.tile([P, 1024], U32, align_bytes=64)
+        wmscl = const.tile([P, 1024], U8, align_bytes=64)
+        mcod = const.tile([P, 512], U32, align_bytes=64)
+        mscl = const.tile([P, 512], U8, align_bytes=64)
+        cT = const.tile([P, 4, 256], F32)
+        bT = const.tile([P, 72], F32)
+        bsum = const.tile([P, 32], F32)
+        bmbc = const.tile([P, 512], F32)
+        midT = const.tile([P, 2, 4, 256], BF16)
+        gm = const.tile([P, 2, 1024], BF16, align_bytes=64)
+
+        load = {"v": 0.0, "s": 0.0}
+        codes = {}
+
+        def copy_out(out_ap, in_ap, eng=None):
+            if eng is None:
+                eng = "v" if load["v"] <= load["s"] else "s"
+            if eng == "v":
+                nc.vector.tensor_copy(out=out_ap, in_=in_ap)
+            else:
+                nc.scalar.copy(out=out_ap, in_=in_ap)
+            load[eng] += 440.0
+
+        def t_bank(srcs):
+            tp = tpp.tile([P, 4, P], F32, tag="tp", name="tp")
+            for q, s in enumerate(srcs):
+                nc.tensor.transpose(tp[:, q, :], s, ident[:])
+            return tp
+
+        def pairs(tp):
+            return tp[:].rearrange("w (a u) p -> w a p u", a=2, u=2)
+
+        def quant(cod_ap, scl_ap, in_ap, cols):
+            nc.vector.quantize_mx(out=cod_ap.bitcast(FP8X4), scales=scl_ap, in_=in_ap)
+            load["v"] += 12.0 + 0.22 * cols
+
+        def unit_T(u):
+            todo = []
+            if u == "C":
+                c3f = c3raw[:].bitcast(F32)
+                for h in range(2):
+                    tp = t_bank(
+                        [
+                            c3f[:, bt, (2 * h + jl) * P : (2 * h + jl + 1) * P]
+                            for jl in range(2)
+                            for bt in range(2)
+                        ]
+                    )
+                    copy_out(
+                        cT[:, 2 * h : 2 * h + 2, :].rearrange("w a b -> w (a b)"),
+                        tp[:].rearrange("w q p -> w (q p)"),
+                    )
+                xf = xraw[:].bitcast(F32)
+                grp = grpp.tile([P, 4096], BF16, tag="grp", name="grp", align_bytes=64)
+                grpf = grp[:].bitcast(F32)
+                tp = t_bank([xf[:, bt, uu * P : (uu + 1) * P] for bt in range(2) for uu in range(2)])
+                copy_out(
+                    grpf[:, 0:512].rearrange("w (a p u) -> w a p u", a=2, p=P, u=2), pairs(tp)
+                )
+                todo.append(lambda: quant(xcod[:], xscl[:], grp[:, 0:1024], 1024))
+                return todo
+            grp = grpp.tile([P, 4096], BF16, tag="grp", name="grp", align_bytes=64)
+            grpf = grp[:].bitcast(F32)
+            if u == "A":
+                for m, src in enumerate((y2raw, h3raw)):
+                    sf = src[:].bitcast(F32)
+                    for bt in range(2):
+                        tp = t_bank([sf[:, bt, q * P : (q + 1) * P] for q in range(4)])
+                        dst = grpf[:, m * 1024 : (m + 1) * 1024].rearrange(
+                            "w (a b u) -> w a b u", a=2, b=B, u=2
+                        )
+                        copy_out(dst[:, :, bt * P : (bt + 1) * P, :], pairs(tp))
+                todo.append(lambda: quant(acod[:], ascl[:], grp[:], 4096))
+                return todo
+            rawf = raws[u][:].bitcast(F32)
+            for c in range(4):
+                tp = t_bank([rawf[:, c * 512 + q * P : c * 512 + (q + 1) * P] for q in range(4)])
+                if u == "M":
+                    dst = grpf.rearrange("w (a m u) -> w a m u", a=2, m=512, u=2)
+                    copy_out(dst[:, :, c * P : (c + 1) * P, :], pairs(tp))
+                else:
+                    copy_out(
+                        grpf[:, c * 512 : (c + 1) * 512].rearrange(
+                            "w (a p u) -> w a p u", a=2, p=P, u=2
+                        ),
+                        pairs(tp),
+                    )
+            if u == "D":
+                todo.append(lambda: quant(dcod[:], dscl[:], grp[:], 4096))
+            elif u == "M":
+                todo.append(lambda: quant(wmcod[:], wmscl[:], grp[:], 4096))
+            else:
+
+                def wq():
+                    cod = codp.tile([P, 1024], U32, tag="cod", name="cod", align_bytes=64)
+                    scl = codp.tile([P, 1024], U8, tag="scl", name="scl", align_bytes=64)
+                    quant(cod[:], scl[:], grp[:], 4096)
+                    codes[u] = (cod, scl)
+
+                todo.append(wq)
+            return todo
+
+        def bias_prep():
+            tp = t_bank([braw[:].bitcast(F32)])
+            nc.vector.tensor_copy(out=bT[:], in_=tp[:].bitcast(BF16)[:, 0, 0:72])
+            nc.vector.tensor_tensor(out=bsum[:], in0=bT[:, 0:32], in1=bT[:, 32:64], op=ALU.add)
+            bmp = dpp.tile([P, 512], F32, tag="dp", name="bmp")
+            nc.tensor.matmul(out=bmp[:], lhsT=ones[:], rhs=bmz[:], start=True, stop=True)
+            copy_out(bmbc[:], bmp[:])
+
+        def mx(out_ap, l_cod, l_scl, l0, r_cod, r_scl, r0, n, start, stop):
+            nc.tensor.matmul_mx(
+                out=out_ap,
+                lhsT=l_cod[:, l0 : l0 + P].bitcast(FP8X4),
+                lhsT_scale=l_scl[:, l0 : l0 + P],
+                rhs=r_cod[:, r0 : r0 + n].bitcast(FP8X4),
+                rhs_scale=r_scl[:, r0 : r0 + n],
+                start=start,
+                stop=stop,
+            )
+
+        def mx_part(q):
+            jj, gate = q // 4, q % 4
+            ua = 4 * jj + 2 * (gate // 2)
+            gl = gate % 2
+            gt = gtp.tile([P, 2, B], F32, tag="gt", name="gt")
+            for e in range(2):
+                for m in range(2):
+                    cod, scl = codes[ua + m]
+                    for g in range(2):
+                        mx(
+                            gt[:, e, :], cod, scl, ((gl * 2 + e) * 2 + g) * P,
+                            acod, ascl, m * 512 + g * B, B,
+                            (m == 0 and g == 0), (m == 1 and g == 1),
+                        )
+            return gt
+
+        def d_pass(jj):
+            dt_ = dpp.tile([P, 2, B], F32, tag="dp", name="dpt")
+            for e in range(2):
+                mx(dt_[:, e, :], dcod, dscl, (2 * jj + e) * P, xcod, xscl, 0, B, True, True)
+            return dt_
+
+        st = {"gact": {}, "a": {}, "b": {}, "cn": {}, "tc": {}, "y": {}, "dp": {}}
+
+        def act_part(q, gt):
+            jj, gate = q // 4, q % 4
+            if gate == 0:
+                st["gact"][jj] = gactp.tile([P, 4, 2, B], F32, tag="gact", name="gact")
+            ga = st["gact"][jj]
+            for e in range(2):
+                col = (gate * 4 + jj) * 2 + e
+                nc.scalar.activation(
+                    out=ga[:, gate, e, :],
+                    in_=gt[:, e, :],
+                    func=(AF.Tanh if gate == 2 else AF.Sigmoid),
+                    bias=bsum[:, col : col + 1],
+                    scale=1.0,
+                )
+                load["s"] += 260.0
+
+        def ew_tt(jj, out_ap, in0, in1, op):
+            if jj < EW_GPSIMD_UNTIL:
+                nc.gpsimd.tensor_tensor(out=out_ap, in0=in0, in1=in1, op=op)
+            else:
+                nc.vector.tensor_tensor(out=out_ap, in0=in0, in1=in1, op=op)
+                load["v"] += 480.0
+
+        def ew_a(jj):
+            a_t = ew1.tile([P, 2, B], F32, tag="a", name="a_t")
+            cv = cT[:].bitcast(BF16)[:, jj, :].rearrange("p (b e) -> p e b", e=2)
+            ew_tt(jj, a_t[:], st["gact"][jj][:, 1, :, :], cv, ALU.mult)
+            st["a"][jj] = a_t
+
+        def ew_cn(jj):
+            b_t = ew1.tile([P, 2, B], F32, tag="b", name="b_t")
+            ga = st["gact"][jj]
+            ew_tt(jj, b_t[:], ga[:, 0, :, :], ga[:, 2, :, :], ALU.mult)
+            cn = ew2.tile([P, 2, B], F32, tag="cn", name="cn")
+            ew_tt(jj, cn[:], st["a"][jj][:], b_t[:], ALU.add)
+            st["cn"][jj] = cn
+
+        def act_tanh_c(jj):
+            tc_t = ew1.tile([P, 2, B], F32, tag="tc", name="tc_t")
+            nc.scalar.activation(out=tc_t[:], in_=st["cn"][jj][:], func=AF.Tanh)
+            load["s"] += 445.0
+            st["tc"][jj] = tc_t
+
+        def ew_y_mid(jj):
+            y_t = ew2.tile([P, 2, B], F32, tag="y", name="y_t")
+            ew_tt(jj, y_t[:], st["gact"][jj][:, 3, :, :], st["tc"][jj][:], ALU.mult)
+            st["y"][jj] = y_t
+            g, uu = jj // 2, jj % 2
+            for e in range(2):
+                nc.vector.scalar_tensor_tensor(
+                    out=midT[:, g, 2 * uu + e, :],
+                    in0=st["dp"][jj][:, e, :],
+                    scalar=bT[:, 64 + 2 * jj + e : 65 + 2 * jj + e],
+                    in1=y_t[:, e, :],
+                    op0=ALU.add,
+                    op1=ALU.add,
+                )
+                load["v"] += 270.0
+            if uu == 1:
+                nc.vector.tensor_copy(
+                    out=gm[:, g, :].rearrange("p (b t) -> p b t", t=4),
+                    in_=midT[:, g, :, :].rearrange("p t b -> p b t"),
+                )
+                load["v"] += 530.0
+
+        def quant_mid(g):
+            quant(mcod[:, g * B : (g + 1) * B], mscl[:, g * B : (g + 1) * B], gm[:, g, :], 1024)
+
+        def out_T(jj, bt, eng=None, at_end=False):
+            if at_end:
+                ot = tpp.tile([P, 4, P], F32, tag="tp", name="ot_end")
+            else:
+                ot = otp.tile([P, 4, P], F32, tag="ot", name="ot")
+            for si, src in enumerate((st["y"][jj], st["cn"][jj])):
+                for e in range(2):
+                    nc.tensor.transpose(
+                        ot[:, si * 2 + e, :], src[:, e, bt * P : (bt + 1) * P], ident[:]
+                    )
+            res = resp.tile([P, 2, B], F32, tag="res", name="res")
+            copy_out(
+                res[:].rearrange("b s (p e) -> b s p e", e=2),
+                ot[:].rearrange("b (s e) p -> b s p e", s=2, e=2),
+                eng,
+            )
+            rows = slice(bt * P, (bt + 1) * P)
+            cols = slice(jj * B, (jj + 1) * B)
+            nc.sync.dma_start(out=out_1[rows, cols], in_=res[:, 0, :])
+            nc.sync.dma_start(out=out_2[rows, cols], in_=res[:, 1, :])
+
+        pend_q = []
+        pend_part = []
+        pend_tanh = []
+        pend_out = []
+        pend_qmid = []
+        next_part = 0
+        step = 0
+        nsteps = len(tunits)
+        while next_part < 16 or pend_part or pend_tanh or step < nsteps:
+            tail = step >= nsteps
+            done_gate = None
+            for jj in pend_tanh:
+                act_tanh_c(jj)
+            pend_tanh = []
+            for q, gt in pend_part:
+                act_part(q, gt)
+                done_gate = q
+            pend_part = []
+            for f in pend_q:
+                f()
+            pend_q = []
+            for g in pend_qmid:
+                quant_mid(g)
+            pend_qmid = []
+            if done_gate is not None:
+                jj, gate = done_gate // 4, done_gate % 4
+                if gate == 1:
+                    ew_a(jj)
+                elif gate == 2:
+                    ew_cn(jj)
+                    pend_tanh.append(jj)
+                elif gate == 3:
+                    ew_y_mid(jj)
+                    if jj % 2 == 1:
+                        pend_qmid.append(jj // 2)
+                    pend_out.append((step + 1, jj, 0))
+                    pend_out.append((step + 2, jj, 1))
+            if not tail:
+                u = tunits[step]
+                pend_q = unit_T(u)
+                if u != "A" and u != "C" and nloaded[0] < len(raw_order):
+                    load_raw(raw_order[nloaded[0]])
+                    nloaded[0] += 1
+                if step == 3:
+                    bias_prep()
+            if jj_ready(pend_out, step) and not (tail and next_part >= 16):
+                first = pend_out[0]
+                out_T(first[1], first[2])
+                pend_out = pend_out[1:]
+            if next_part < 16 and pos[2 * (next_part // 2) + 1] + MINLAG <= step:
+                gt = mx_part(next_part)
+                pend_part.append((next_part, gt))
+                if next_part % 4 == 3:
+                    st["dp"][next_part // 4] = d_pass(next_part // 4)
+                next_part += 1
+            step += 1
+
+        for g in pend_qmid:
+            quant_mid(g)
+        nc.scalar.activation(out=dum2[:], in_=dum[:], func=AF.Exp)
+        for item in pend_out:
+            out_T(item[1], item[2], "s", True)
+        mps = []
+        for bt in range(2):
+            mp = tpp.tile([P, 512], F32, tag="tp", name="mp")
+            for g in range(2):
+                mx(
+                    mp[:], mcod, mscl, g * B + bt * P, wmcod, wmscl, g * 512, 512,
+                    g == 0, g == 1,
+                )
+            mps.append(mp)
+        ssum = const.tile([P, 2], F32)
+        lsum = const.tile([P, 2], F32)
+        mots = []
+        nmxs = []
+        for bt in range(2):
+            mot = const.tile([P, 512], F32, name="mot%d" % bt)
+            nmx = const.tile([P, 1], F32, name="nmx%d" % bt)
+            ex = const.tile([P, 512], F32, name="ex%d" % bt)
+            nc.vector.tensor_tensor(out=mot[:], in0=mps[bt][:], in1=bmbc[:], op=ALU.add)
+            nc.vector.tensor_reduce(out=nmx[:], in_=mot[:], axis=AX.X, op=ALU.max, negate=True)
+            nc.scalar.activation(
+                out=ex[:], in_=mot[:], func=AF.Exp, bias=nmx[:, 0:1], scale=1.0,
+                accum_out=ssum[:, bt : bt + 1],
+            )
+            mots.append(mot)
+            nmxs.append(nmx)
+        nc.scalar.activation(out=lsum[:], in_=ssum[:], func=AF.Ln)
+        for bt in range(2):
+            fin = const.tile([P, 512], F32, name="fin%d" % bt)
+            nc.vector.tensor_scalar(
+                out=fin[:], in0=mots[bt][:], scalar1=nmxs[bt][:, 0:1],
+                scalar2=lsum[:, bt : bt + 1], op0=ALU.add, op1=ALU.subtract,
+            )
+            nc.sync.dma_start(out=out_0[bt * P : (bt + 1) * P, :], in_=fin[:])
+
+
+def jj_ready(pend_out, step):
+    return len(pend_out) > 0 and pend_out[0][0] <= step

@@ -16,9 +16,22 @@ P = 128
 B = 256
 FLOPS = 2 * 256 * (4096 * 2048 + 1024 * 512 + 512 * 1024)
 
-EW_GPSIMD_UNTIL = 3
-MINLAG = 2
-RAW_BUFS = 8
+LAG = 2
+LAG1_FROM = 16
+HALFQ = True
+RAW_BUFS = 9
+TUNITS = ["A", 0, 1, 2, 3, 4, 5, 6, 7, 8, 9, 10, 11, 12, 13, 14, 15]
+LOADS = ["A", 0, 1, "C", 2, 3, 4, "D", 5, 6, 7, 8, "M", 9, 10, 11, 12, 13, 14, 15]
+EXTRA = {
+    0: [("bias", 0)], 2: [("c3", 0)], 3: [("c3", 1)], 4: [("x", 0)],
+    5: [("D", 0)], 6: [("D", 1)], 7: [("D", 2)], 8: [("D", 3)],
+    9: [("M", 0)], 10: [("M", 1)], 11: [("M", 2)], 12: [("M", 3)],
+}
+WARM = 6
+DUMMY_AFTER_BANK = {"A": [0, 1, 2, 3], 0: [1, 3], 1: [1, 3]}
+EW_GPSIMD_UNTIL = 0
+TANH_DELAY = 1
+MID_DELAY = 1
 
 
 def tile_network_pb_kernel(
@@ -29,25 +42,27 @@ def tile_network_pb_kernel(
         const = ctx.enter_context(tc.tile_pool(name="const", bufs=1))
         rawp = ctx.enter_context(tc.tile_pool(name="rawp", bufs=RAW_BUFS))
         grpp = ctx.enter_context(tc.tile_pool(name="grpp", bufs=3))
-        codp = ctx.enter_context(tc.tile_pool(name="codp", bufs=6))
+        grpx = ctx.enter_context(tc.tile_pool(name="grpx", bufs=1))
+        codp = ctx.enter_context(tc.tile_pool(name="codp", bufs=4))
         gactp = ctx.enter_context(tc.tile_pool(name="gactp", bufs=2))
         ew1 = ctx.enter_context(tc.tile_pool(name="ew1", bufs=1))
-        ew2 = ctx.enter_context(tc.tile_pool(name="ew2", bufs=2))
-        resp = ctx.enter_context(tc.tile_pool(name="resp", bufs=3))
-        tpp = ctx.enter_context(tc.psum_pool(name="tpp", bufs=4))
+        ew4 = ctx.enter_context(tc.tile_pool(name="ew4", bufs=4))
+        resp = ctx.enter_context(tc.tile_pool(name="resp", bufs=8))
+        tpp = ctx.enter_context(tc.psum_pool(name="tpp", bufs=5))
         gtp = ctx.enter_context(tc.psum_pool(name="gtp", bufs=2))
-        otp = ctx.enter_context(tc.psum_pool(name="otp", bufs=1))
         dpp = ctx.enter_context(tc.psum_pool(name="dpp", bufs=1))
         ctx.enter_context(tc.manual_schedule())
 
+        ones = const.tile([P, P], BF16)
+        zz = const.tile([P, 512], BF16)
         braw = const.tile([P, 256], BF16)
         bmz = const.tile([P, 512], BF16)
-        ones = const.tile([P, P], BF16)
         dum = const.tile([P, 1], F32)
         dum2 = const.tile([P, 1], F32)
+        nc.vector.memset(ones[:], 1.0)
+        nc.vector.memset(zz[:], 0.0)
         nc.vector.memset(braw[:], 0.0)
         nc.vector.memset(bmz[:], 0.0)
-        nc.vector.memset(ones[:], 1.0)
         nc.vector.memset(dum[:], 0.0)
         nc.scalar.dma_start(out=braw[0:16, :], in_=bih3.rearrange("(r c) -> r c", c=256))
         nc.scalar.dma_start(out=braw[16:32, :], in_=bhh3.rearrange("(r c) -> r c", c=256))
@@ -57,18 +72,36 @@ def tile_network_pb_kernel(
         ident = const.tile([P, P], F32)
         make_identity(nc, ident[:])
 
-        y2raw = const.tile([P, 2, 1024], BF16)
-        h3raw = const.tile([P, 2, 1024], BF16)
-        c3raw = const.tile([P, 2, 1024], BF16)
-        xraw = const.tile([P, 2, 512], BF16)
+        dmy = dpp.tile([P, 512], F32, tag="dp", name="dmy")
+
+        def dummy():
+            nc.tensor.matmul(out=dmy[:], lhsT=ones[:], rhs=zz[:], start=True, stop=True)
+
         wviews = [
-            w.rearrange("(g j p e) k -> j p g (e k)", g=4, j=4, p=P, e=2) for w in (Wih3, Whh3)
+            w.rearrange("(g j p e) k -> g j p (e k)", g=4, j=4, p=P, e=2) for w in (Wih3, Whh3)
         ]
         raws = {}
+        released = set()
+        nloaded = [0]
 
-        def load_raw(key):
+        def load_unit(key):
             raw = rawp.tile([P, 4096], BF16, tag="raw", name="raw")
-            if key == "D":
+            if key == "A":
+                for m, src in enumerate((y2, h3)):
+                    nc.sync.dma_start(
+                        out=raw[:, m * 2048 : (m + 1) * 2048].rearrange("p (t k) -> p t k", t=2),
+                        in_=src.rearrange("(t p) k -> p t k", p=P),
+                    )
+            elif key == "C":
+                nc.sync.dma_start(
+                    out=raw[:, 0:2048].rearrange("p (t k) -> p t k", t=2),
+                    in_=c3.rearrange("(t p) k -> p t k", p=P),
+                )
+                nc.sync.dma_start(
+                    out=raw[:, 2048:3072].rearrange("p (t k) -> p t k", t=2),
+                    in_=x.rearrange("(t p) k -> p t k", p=P),
+                )
+            elif key == "D":
                 nc.sync.dma_start(
                     out=raw[:].rearrange("p (j f) -> p j f", j=4),
                     in_=Wd.rearrange("(j p e) k -> p j (e k)", j=4, p=P, e=2),
@@ -79,28 +112,22 @@ def tile_network_pb_kernel(
                     in_=Wm.rearrange("(a p) k -> p a k", p=P),
                 )
             else:
-                jj, gp, m = key // 4, (key % 4) // 2, key % 2
-                nc.sync.dma_start(
-                    out=raw[:].rearrange("p (g f) -> p g f", g=2),
-                    in_=wviews[m][jj][:, 2 * gp : 2 * gp + 2, :],
-                )
+                for m in range(2):
+                    nc.sync.dma_start(
+                        out=raw[:, m * 2048 : (m + 1) * 2048], in_=wviews[m][key % 4, key // 4]
+                    )
             raws[key] = raw
 
-        tunits = ["A", 0, 1, 2, 3, "C", "D", 4, 5, 6, 7, 8, 9, 10, 11, "M", 12, 13, 14, 15]
-        raw_order = [u for u in tunits if u != "A" and u != "C"]
-        pos = {}
-        for i, u in enumerate(tunits):
-            pos[u] = i
+        def load_more():
+            while nloaded[0] < len(LOADS) and (
+                nloaded[0] < RAW_BUFS or LOADS[nloaded[0] - RAW_BUFS] in released
+            ):
+                load_unit(LOADS[nloaded[0]])
+                nloaded[0] += 1
 
-        nc.sync.dma_start(out=y2raw[:], in_=y2.rearrange("(t p) k -> p t k", p=P))
-        nc.sync.dma_start(out=h3raw[:], in_=h3.rearrange("(t p) k -> p t k", p=P))
-        for key in raw_order[0:4]:
-            load_raw(key)
-        nc.sync.dma_start(out=c3raw[:], in_=c3.rearrange("(t p) k -> p t k", p=P))
-        nc.sync.dma_start(out=xraw[:], in_=x.rearrange("(t p) k -> p t k", p=P))
-        for key in raw_order[4:RAW_BUFS]:
-            load_raw(key)
-        nloaded = [RAW_BUFS]
+        load_more()
+        for i in range(WARM):
+            dummy()
 
         acod = const.tile([P, 1024], U32, align_bytes=64)
         ascl = const.tile([P, 1024], U8, align_bytes=64)
@@ -112,6 +139,7 @@ def tile_network_pb_kernel(
         wmscl = const.tile([P, 1024], U8, align_bytes=64)
         mcod = const.tile([P, 512], U32, align_bytes=64)
         mscl = const.tile([P, 512], U8, align_bytes=64)
+        xgrp = const.tile([P, 1024], BF16, align_bytes=64)
         cT = const.tile([P, 4, 256], F32)
         bT = const.tile([P, 72], F32)
         bsum = const.tile([P, 32], F32)
@@ -121,6 +149,8 @@ def tile_network_pb_kernel(
 
         load = {"v": 0.0, "s": 0.0}
         codes = {}
+        done = set()
+        big = {}
 
         def copy_out(out_ap, in_ap, eng=None):
             if eng is None:
@@ -140,83 +170,112 @@ def tile_network_pb_kernel(
         def pairs(tp):
             return tp[:].rearrange("w (a u) p -> w a p u", a=2, u=2)
 
-        def quant(cod_ap, scl_ap, in_ap, cols):
+        def pair_dst(ap):
+            return ap.rearrange("w (a p u) -> w a p u", a=2, p=P, u=2)
+
+        def quant(cod_ap, scl_ap, in_ap, cols, flag=None):
             nc.vector.quantize_mx(out=cod_ap.bitcast(FP8X4), scales=scl_ap, in_=in_ap)
             load["v"] += 12.0 + 0.22 * cols
+            if flag is not None:
+                done.add(flag)
 
         def unit_T(u):
             todo = []
-            if u == "C":
-                c3f = c3raw[:].bitcast(F32)
-                for h in range(2):
-                    tp = t_bank(
-                        [
-                            c3f[:, bt, (2 * h + jl) * P : (2 * h + jl + 1) * P]
-                            for jl in range(2)
-                            for bt in range(2)
-                        ]
-                    )
-                    copy_out(
-                        cT[:, 2 * h : 2 * h + 2, :].rearrange("w a b -> w (a b)"),
-                        tp[:].rearrange("w q p -> w (q p)"),
-                    )
-                xf = xraw[:].bitcast(F32)
-                grp = grpp.tile([P, 4096], BF16, tag="grp", name="grp", align_bytes=64)
-                grpf = grp[:].bitcast(F32)
-                tp = t_bank([xf[:, bt, uu * P : (uu + 1) * P] for bt in range(2) for uu in range(2)])
-                copy_out(
-                    grpf[:, 0:512].rearrange("w (a p u) -> w a p u", a=2, p=P, u=2), pairs(tp)
-                )
-                todo.append(lambda: quant(xcod[:], xscl[:], grp[:, 0:1024], 1024))
-                return todo
+            rawf = raws[u][:].bitcast(F32)
             grp = grpp.tile([P, 4096], BF16, tag="grp", name="grp", align_bytes=64)
             grpf = grp[:].bitcast(F32)
+            dums = DUMMY_AFTER_BANK.get(u, [])
             if u == "A":
-                for m, src in enumerate((y2raw, h3raw)):
-                    sf = src[:].bitcast(F32)
-                    for bt in range(2):
-                        tp = t_bank([sf[:, bt, q * P : (q + 1) * P] for q in range(4)])
-                        dst = grpf[:, m * 1024 : (m + 1) * 1024].rearrange(
-                            "w (a b u) -> w a b u", a=2, b=B, u=2
-                        )
-                        copy_out(dst[:, :, bt * P : (bt + 1) * P, :], pairs(tp))
-                todo.append(lambda: quant(acod[:], ascl[:], grp[:], 4096))
-                return todo
-            rawf = raws[u][:].bitcast(F32)
-            for c in range(4):
-                tp = t_bank([rawf[:, c * 512 + q * P : c * 512 + (q + 1) * P] for q in range(4)])
-                if u == "M":
-                    dst = grpf.rearrange("w (a m u) -> w a m u", a=2, m=512, u=2)
-                    copy_out(dst[:, :, c * P : (c + 1) * P, :], pairs(tp))
-                else:
-                    copy_out(
-                        grpf[:, c * 512 : (c + 1) * 512].rearrange(
-                            "w (a p u) -> w a p u", a=2, p=P, u=2
-                        ),
-                        pairs(tp),
+                for c in range(4):
+                    m, bt = c // 2, c % 2
+                    w0 = m * 1024 + bt * 512
+                    tp = t_bank([rawf[:, w0 + q * P : w0 + (q + 1) * P] for q in range(4)])
+                    dst = grpf[:, m * 1024 : (m + 1) * 1024].rearrange(
+                        "w (a b u) -> w a b u", a=2, b=B, u=2
                     )
-            if u == "D":
-                todo.append(lambda: quant(dcod[:], dscl[:], grp[:], 4096))
-            elif u == "M":
-                todo.append(lambda: quant(wmcod[:], wmscl[:], grp[:], 4096))
+                    copy_out(dst[:, :, bt * P : (bt + 1) * P, :], pairs(tp))
+                    if c in dums:
+                        dummy()
+                    if c == 2:
+                        quant(acod[:, 0:512], ascl[:, 0:512], grp[:, 0:2048], 2048)
+                todo.append(
+                    lambda: quant(acod[:, 512:1024], ascl[:, 512:1024], grp[:, 2048:4096], 2048)
+                )
+                return todo
+            cod = codp.tile([P, 1024], U32, tag="cod", name="cod", align_bytes=64)
+            scl = codp.tile([P, 1024], U8, tag="scl", name="scl", align_bytes=64)
+            codes[u] = (cod, scl)
+            order = [0, 2, 1, 3] if u == 0 else [0, 1, 2, 3]
+            for n, c in enumerate(order):
+                e, m = c // 2, c % 2
+                w0 = m * 1024 + e * 512
+                tp = t_bank([rawf[:, w0 + q * P : w0 + (q + 1) * P] for q in range(4)])
+                copy_out(pair_dst(grpf[:, c * 512 : (c + 1) * 512]), pairs(tp))
+                if n in dums:
+                    dummy()
+                if HALFQ and u != 0 and n == 2:
+                    quant(cod[:, 0:512], scl[:, 0:512], grp[:, 0:2048], 2048)
+            if HALFQ and u != 0:
+                todo.append(
+                    lambda: quant(cod[:, 512:1024], scl[:, 512:1024], grp[:, 2048:4096], 2048)
+                )
             else:
-
-                def wq():
-                    cod = codp.tile([P, 1024], U32, tag="cod", name="cod", align_bytes=64)
-                    scl = codp.tile([P, 1024], U8, tag="scl", name="scl", align_bytes=64)
-                    quant(cod[:], scl[:], grp[:], 4096)
-                    codes[u] = (cod, scl)
-
-                todo.append(wq)
+                todo.append(lambda: quant(cod[:], scl[:], grp[:], 4096))
             return todo
 
-        def bias_prep():
-            tp = t_bank([braw[:].bitcast(F32)])
-            nc.vector.tensor_copy(out=bT[:], in_=tp[:].bitcast(BF16)[:, 0, 0:72])
-            nc.vector.tensor_tensor(out=bsum[:], in0=bT[:, 0:32], in1=bT[:, 32:64], op=ALU.add)
-            bmp = dpp.tile([P, 512], F32, tag="dp", name="bmp")
-            nc.tensor.matmul(out=bmp[:], lhsT=ones[:], rhs=bmz[:], start=True, stop=True)
-            copy_out(bmbc[:], bmp[:])
+        def extra_bank(kind, i):
+            if kind == "bias":
+                tp = t_bank([braw[:].bitcast(F32)])
+                nc.vector.tensor_copy(out=bT[:], in_=tp[:].bitcast(BF16)[:, 0, 0:72])
+                nc.vector.tensor_tensor(out=bsum[:], in0=bT[:, 0:32], in1=bT[:, 32:64], op=ALU.add)
+                bmp = tpp.tile([P, 512], F32, tag="tp", name="bmp")
+                nc.tensor.matmul(out=bmp[:], lhsT=ones[:], rhs=bmz[:], start=True, stop=True)
+                copy_out(bmbc[:], bmp[:])
+                return []
+            if kind == "c3":
+                cf = raws["C"][:].bitcast(F32)
+                tp = t_bank(
+                    [
+                        cf[:, bt * 512 + (2 * i + jl) * P : bt * 512 + (2 * i + jl + 1) * P]
+                        for jl in range(2)
+                        for bt in range(2)
+                    ]
+                )
+                copy_out(
+                    cT[:, 2 * i : 2 * i + 2, :].rearrange("w a b -> w (a b)"),
+                    tp[:].rearrange("w q p -> w (q p)"),
+                )
+                done.add(("c3", i))
+                return []
+            if kind == "x":
+                cf = raws["C"][:].bitcast(F32)
+                tp = t_bank(
+                    [
+                        cf[:, 1024 + bt * 256 + uu * P : 1024 + bt * 256 + (uu + 1) * P]
+                        for bt in range(2)
+                        for uu in range(2)
+                    ]
+                )
+                copy_out(pair_dst(xgrp[:].bitcast(F32)), pairs(tp))
+                released.add("C")
+                return [lambda: quant(xcod[:], xscl[:], xgrp[:], 1024, "qx")]
+            rawf = raws[kind][:].bitcast(F32)
+            if i == 0:
+                big[kind] = grpx.tile([P, 4096], BF16, tag="big", name="big", align_bytes=64)
+            grp = big[kind]
+            grpf = grp[:].bitcast(F32)
+            tp = t_bank([rawf[:, i * 512 + q * P : i * 512 + (q + 1) * P] for q in range(4)])
+            if kind == "M":
+                dst = grpf.rearrange("w (a m u) -> w a m u", a=2, m=512, u=2)
+                copy_out(dst[:, :, i * P : (i + 1) * P, :], pairs(tp))
+            else:
+                copy_out(pair_dst(grpf[:, i * 512 : (i + 1) * 512]), pairs(tp))
+            if i < 3:
+                return []
+            released.add(kind)
+            if kind == "D":
+                return [lambda: quant(dcod[:], dscl[:], grp[:], 4096, "qD")]
+            return [lambda: quant(wmcod[:], wmscl[:], grp[:], 4096, "qM")]
 
         def mx(out_ap, l_cod, l_scl, l0, r_cod, r_scl, r0, n, start, stop):
             nc.tensor.matmul_mx(
@@ -229,20 +288,20 @@ def tile_network_pb_kernel(
                 stop=stop,
             )
 
+        def mx_group(out_ap, q, e):
+            cod, scl = codes[q]
+            for m in range(2):
+                for g in range(2):
+                    mx(
+                        out_ap, cod, scl, ((e * 2 + m) * 2 + g) * P,
+                        acod, ascl, m * 512 + g * B, B,
+                        (m == 0 and g == 0), (m == 1 and g == 1),
+                    )
+
         def mx_part(q):
-            jj, gate = q // 4, q % 4
-            ua = 4 * jj + 2 * (gate // 2)
-            gl = gate % 2
             gt = gtp.tile([P, 2, B], F32, tag="gt", name="gt")
             for e in range(2):
-                for m in range(2):
-                    cod, scl = codes[ua + m]
-                    for g in range(2):
-                        mx(
-                            gt[:, e, :], cod, scl, ((gl * 2 + e) * 2 + g) * P,
-                            acod, ascl, m * 512 + g * B, B,
-                            (m == 0 and g == 0), (m == 1 and g == 1),
-                        )
+                mx_group(gt[:, e, :], q, e)
             return gt
 
         def d_pass(jj):
@@ -253,21 +312,23 @@ def tile_network_pb_kernel(
 
         st = {"gact": {}, "a": {}, "b": {}, "cn": {}, "tc": {}, "y": {}, "dp": {}}
 
-        def act_part(q, gt):
+        def act_gate(q, e, in_ap):
             jj, gate = q // 4, q % 4
-            if gate == 0:
-                st["gact"][jj] = gactp.tile([P, 4, 2, B], F32, tag="gact", name="gact")
-            ga = st["gact"][jj]
+            col = (gate * 4 + jj) * 2 + e
+            nc.scalar.activation(
+                out=st["gact"][jj][:, gate, e, :],
+                in_=in_ap,
+                func=(AF.Tanh if gate == 2 else AF.Sigmoid),
+                bias=bsum[:, col : col + 1],
+                scale=1.0,
+            )
+            load["s"] += 260.0
+
+        def act_part(q, gt):
+            if q % 4 == 0:
+                st["gact"][q // 4] = gactp.tile([P, 4, 2, B], F32, tag="gact", name="gact")
             for e in range(2):
-                col = (gate * 4 + jj) * 2 + e
-                nc.scalar.activation(
-                    out=ga[:, gate, e, :],
-                    in_=gt[:, e, :],
-                    func=(AF.Tanh if gate == 2 else AF.Sigmoid),
-                    bias=bsum[:, col : col + 1],
-                    scale=1.0,
-                )
-                load["s"] += 260.0
+                act_gate(q, e, gt[:, e, :])
 
         def ew_tt(jj, out_ap, in0, in1, op):
             if jj < EW_GPSIMD_UNTIL:
@@ -286,7 +347,7 @@ def tile_network_pb_kernel(
             b_t = ew1.tile([P, 2, B], F32, tag="b", name="b_t")
             ga = st["gact"][jj]
             ew_tt(jj, b_t[:], ga[:, 0, :, :], ga[:, 2, :, :], ALU.mult)
-            cn = ew2.tile([P, 2, B], F32, tag="cn", name="cn")
+            cn = ew4.tile([P, 2, B], F32, tag="cn", name="cn")
             ew_tt(jj, cn[:], st["a"][jj][:], b_t[:], ALU.add)
             st["cn"][jj] = cn
 
@@ -296,41 +357,44 @@ def tile_network_pb_kernel(
             load["s"] += 445.0
             st["tc"][jj] = tc_t
 
-        def ew_y_mid(jj):
-            y_t = ew2.tile([P, 2, B], F32, tag="y", name="y_t")
+        def ew_y(jj):
+            y_t = ew4.tile([P, 2, B], F32, tag="y", name="y_t")
             ew_tt(jj, y_t[:], st["gact"][jj][:, 3, :, :], st["tc"][jj][:], ALU.mult)
             st["y"][jj] = y_t
+
+        def mid_half(jj, e):
+            nc.vector.scalar_tensor_tensor(
+                out=midT[:, jj // 2, 2 * (jj % 2) + e, :],
+                in0=st["dp"][jj][:, e, :],
+                scalar=bT[:, 64 + 2 * jj + e : 65 + 2 * jj + e],
+                in1=st["y"][jj][:, e, :],
+                op0=ALU.add,
+                op1=ALU.add,
+            )
+            load["v"] += 270.0
+
+        def mid_regroup(jj):
             g, uu = jj // 2, jj % 2
-            for e in range(2):
-                nc.vector.scalar_tensor_tensor(
-                    out=midT[:, g, 2 * uu + e, :],
-                    in0=st["dp"][jj][:, e, :],
-                    scalar=bT[:, 64 + 2 * jj + e : 65 + 2 * jj + e],
-                    in1=y_t[:, e, :],
-                    op0=ALU.add,
-                    op1=ALU.add,
-                )
-                load["v"] += 270.0
-            if uu == 1:
-                nc.vector.tensor_copy(
-                    out=gm[:, g, :].rearrange("p (b t) -> p b t", t=4),
-                    in_=midT[:, g, :, :].rearrange("p t b -> p b t"),
-                )
-                load["v"] += 530.0
+            nc.vector.tensor_copy(
+                out=gm[:, g, :].rearrange("p (b t) -> p b t", t=4)[:, :, 2 * uu : 2 * uu + 2],
+                in_=midT[:, g, 2 * uu : 2 * uu + 2, :].rearrange("p t b -> p b t"),
+            )
+            load["v"] += 330.0
 
         def quant_mid(g):
             quant(mcod[:, g * B : (g + 1) * B], mscl[:, g * B : (g + 1) * B], gm[:, g, :], 1024)
 
-        def out_T(jj, bt, eng=None, at_end=False):
-            if at_end:
-                ot = tpp.tile([P, 4, P], F32, tag="tp", name="ot_end")
-            else:
-                ot = otp.tile([P, 4, P], F32, tag="ot", name="ot")
+        def out_T(jj, bt):
+            ot = tpp.tile([P, 4, P], F32, tag="tp", name="ot")
             for si, src in enumerate((st["y"][jj], st["cn"][jj])):
                 for e in range(2):
                     nc.tensor.transpose(
                         ot[:, si * 2 + e, :], src[:, e, bt * P : (bt + 1) * P], ident[:]
                     )
+            return (jj, bt, ot)
+
+        def out_store(item, eng):
+            jj, bt, ot = item
             res = resp.tile([P, 2, B], F32, tag="res", name="res")
             copy_out(
                 res[:].rearrange("b s (p e) -> b s p e", e=2),
@@ -342,85 +406,149 @@ def tile_network_pb_kernel(
             nc.sync.dma_start(out=out_1[rows, cols], in_=res[:, 0, :])
             nc.sync.dma_start(out=out_2[rows, cols], in_=res[:, 1, :])
 
+        pos = {}
+        for i, u in enumerate(TUNITS):
+            pos[u] = i
         pend_q = []
         pend_part = []
-        pend_tanh = []
-        pend_out = []
-        pend_qmid = []
+        due = {}
         next_part = 0
-        step = 0
-        nsteps = len(tunits)
-        while next_part < 16 or pend_part or pend_tanh or step < nsteps:
-            tail = step >= nsteps
-            done_gate = None
-            for jj in pend_tanh:
-                act_tanh_c(jj)
-            pend_tanh = []
+        step = -1
+        while step < len(TUNITS) - 1 or ("mid", 2) not in done or "qmid0" not in done:
+            step += 1
+            u = TUNITS[step] if step < len(TUNITS) else None
             for q, gt in pend_part:
                 act_part(q, gt)
-                done_gate = q
+                done.add(("act", q))
             pend_part = []
+            for jj in range(3):
+                if due.get(("tanh", jj), 99) <= step and ("tanh", jj) not in done:
+                    act_tanh_c(jj)
+                    done.add(("tanh", jj))
             for f in pend_q:
                 f()
             pend_q = []
-            for g in pend_qmid:
-                quant_mid(g)
-            pend_qmid = []
-            if done_gate is not None:
-                jj, gate = done_gate // 4, done_gate % 4
-                if gate == 1:
+            if due.get("qmid0", 99) <= step and "qmid0" not in done:
+                quant_mid(0)
+                done.add("qmid0")
+            for jj in range(3):
+                if due.get(("mid", jj), 99) <= step and ("mid", jj) not in done and jj in st["dp"]:
+                    mid_half(jj, 0)
+                    mid_half(jj, 1)
+                    mid_regroup(jj)
+                    done.add(("mid", jj))
+                    if jj == 1:
+                        due["qmid0"] = step + 1
+            for jj in range(4):
+                if (
+                    ("act", 4 * jj + 1) in done
+                    and ("c3", jj // 2) in done
+                    and ("A", jj) not in done
+                ):
                     ew_a(jj)
-                elif gate == 2:
+                    done.add(("A", jj))
+                if jj == 3:
+                    continue
+                if ("act", 4 * jj + 2) in done and ("A", jj) in done and ("cn", jj) not in done:
                     ew_cn(jj)
-                    pend_tanh.append(jj)
-                elif gate == 3:
-                    ew_y_mid(jj)
-                    if jj % 2 == 1:
-                        pend_qmid.append(jj // 2)
-                    pend_out.append((step + 1, jj, 0))
-                    pend_out.append((step + 2, jj, 1))
-            if not tail:
-                u = tunits[step]
+                    done.add(("cn", jj))
+                    due[("tanh", jj)] = step + TANH_DELAY
+                if ("tanh", jj) in done and ("act", 4 * jj + 3) in done and ("y", jj) not in done:
+                    ew_y(jj)
+                    done.add(("y", jj))
+                    due[("mid", jj)] = step + MID_DELAY
+            if u is not None:
                 pend_q = unit_T(u)
-                if u != "A" and u != "C" and nloaded[0] < len(raw_order):
-                    load_raw(raw_order[nloaded[0]])
-                    nloaded[0] += 1
-                if step == 3:
-                    bias_prep()
-            if jj_ready(pend_out, step) and not (tail and next_part >= 16):
-                first = pend_out[0]
-                out_T(first[1], first[2])
-                pend_out = pend_out[1:]
-            if next_part < 16 and pos[2 * (next_part // 2) + 1] + MINLAG <= step:
-                gt = mx_part(next_part)
-                pend_part.append((next_part, gt))
-                if next_part % 4 == 3:
-                    st["dp"][next_part // 4] = d_pass(next_part // 4)
+                released.add(u)
+                for kind, i in EXTRA.get(u, []):
+                    pend_q = pend_q + extra_bank(kind, i)
+                load_more()
+            while (
+                next_part < 15
+                and len(pend_part) < 2
+                and pos[next_part] + (LAG if next_part < LAG1_FROM else 1) <= step
+            ):
+                pend_part.append((next_part, mx_part(next_part)))
                 next_part += 1
-            step += 1
+            for jj in range(4):
+                if (
+                    jj not in st["dp"]
+                    and "qD" in done
+                    and "qx" in done
+                    and next_part > 4 * jj + 2
+                    and (jj == 0 or ("mid", jj - 1) in done)
+                ):
+                    st["dp"][jj] = d_pass(jj)
 
-        for g in pend_qmid:
-            quant_mid(g)
-        nc.scalar.activation(out=dum2[:], in_=dum[:], func=AF.Exp)
-        for item in pend_out:
-            out_T(item[1], item[2], "s", True)
+        for f in pend_q:
+            f()
+        while pend_part or next_part < 15:
+            for q, gt in pend_part:
+                act_part(q, gt)
+                if q == 13:
+                    ew_a(3)
+            pend_part = []
+            if next_part < 15:
+                pend_part.append((next_part, mx_part(next_part)))
+                next_part += 1
+        for jj in range(3):
+            assert ("mid", jj) in done
+        assert "qmid0" in done and "qM" in done
+        if 3 not in st["dp"]:
+            st["dp"][3] = d_pass(3)
+        o_banks = []
+        for e in range(2):
+            ob = tpp.tile([P, B], F32, tag="tp", name="ob")
+            mx_group(ob[:], 15, e)
+            o_banks.append(ob)
+        ga = st["gact"][3]
+        b_t = ew1.tile([P, 2, B], F32, tag="b", name="b_t")
+        cn = ew4.tile([P, 2, B], F32, tag="cn", name="cn")
+        tc_t = ew1.tile([P, 2, B], F32, tag="tc", name="tc_t")
+        y_t = ew4.tile([P, 2, B], F32, tag="y", name="y_t")
+        st["cn"][3] = cn
+        st["y"][3] = y_t
+        for e in range(2):
+            nc.vector.tensor_tensor(
+                out=b_t[:, e, :], in0=ga[:, 0, e, :], in1=ga[:, 2, e, :], op=ALU.mult
+            )
+            nc.vector.tensor_tensor(
+                out=cn[:, e, :], in0=st["a"][3][:, e, :], in1=b_t[:, e, :], op=ALU.add
+            )
+        for e in range(2):
+            act_gate(15, e, o_banks[e][:])
+            nc.scalar.activation(out=tc_t[:, e, :], in_=cn[:, e, :], func=AF.Tanh)
         mps = []
         for bt in range(2):
-            mp = tpp.tile([P, 512], F32, tag="tp", name="mp")
-            for g in range(2):
-                mx(
-                    mp[:], mcod, mscl, g * B + bt * P, wmcod, wmscl, g * 512, 512,
-                    g == 0, g == 1,
-                )
+            mp = gtp.tile([P, 512], F32, tag="gt", name="mp")
+            mx(mp[:], mcod, mscl, bt * P, wmcod, wmscl, 0, 512, True, False)
             mps.append(mp)
+        outs = [(jj, bt) for jj in range(4) for bt in range(2)]
+        banks = [out_T(jj, bt) for jj, bt in outs[0:3]]
+        for e in range(2):
+            nc.vector.tensor_tensor(
+                out=y_t[:, e, :], in0=ga[:, 3, e, :], in1=tc_t[:, e, :], op=ALU.mult
+            )
+            mid_half(3, e)
+        mid_regroup(3)
+        quant_mid(1)
+        for item in banks:
+            out_store(item, "s")
+        banks = [out_T(jj, bt) for jj, bt in outs[3:5]]
+        out_store(banks[0], "s")
+        nc.scalar.activation(out=dum2[:], in_=dum[:], func=AF.Exp)
+        for bt in range(2):
+            mx(mps[bt][:], mcod, mscl, B + bt * P, wmcod, wmscl, 512, 512, False, True)
+        out_store(banks[1], "v")
+        banks = [out_T(jj, bt) for jj, bt in outs[5:8]]
         ssum = const.tile([P, 2], F32)
         lsum = const.tile([P, 2], F32)
+        ex = const.tile([P, 512], F32)
         mots = []
         nmxs = []
         for bt in range(2):
             mot = const.tile([P, 512], F32, name="mot%d" % bt)
             nmx = const.tile([P, 1], F32, name="nmx%d" % bt)
-            ex = const.tile([P, 512], F32, name="ex%d" % bt)
             nc.vector.tensor_tensor(out=mot[:], in0=mps[bt][:], in1=bmbc[:], op=ALU.add)
             nc.vector.tensor_reduce(out=nmx[:], in_=mot[:], axis=AX.X, op=ALU.max, negate=True)
             nc.scalar.activation(
@@ -430,14 +558,11 @@ def tile_network_pb_kernel(
             mots.append(mot)
             nmxs.append(nmx)
         nc.scalar.activation(out=lsum[:], in_=ssum[:], func=AF.Ln)
+        for item in banks:
+            out_store(item, "v")
         for bt in range(2):
-            fin = const.tile([P, 512], F32, name="fin%d" % bt)
             nc.vector.tensor_scalar(
-                out=fin[:], in0=mots[bt][:], scalar1=nmxs[bt][:, 0:1],
+                out=mots[bt][:], in0=mots[bt][:], scalar1=nmxs[bt][:, 0:1],
                 scalar2=lsum[:, bt : bt + 1], op0=ALU.add, op1=ALU.subtract,
             )
-            nc.sync.dma_start(out=out_0[bt * P : (bt + 1) * P, :], in_=fin[:])
-
-
-def jj_ready(pend_out, step):
-    return len(pend_out) > 0 and pend_out[0][0] <= step
+            nc.sync.dma_start(out=out_0[bt * P : (bt + 1) * P, :], in_=mots[bt][:])

@@ -14,24 +14,17 @@ AX = mybir.AxisListType
 
 P = 128
 B = 256
+UNITS = 16
 FLOPS = 2 * 256 * (4096 * 2048 + 1024 * 512 + 512 * 1024)
 
-LAG = 2
-LAG1_FROM = 16
-HALFQ = True
-RAW_BUFS = 9
-TUNITS = ["A", 0, 1, 2, 3, 4, 5, 6, 7, 8, 9, 10, 11, 12, 13, 14, 15]
-LOADS = ["A", 0, 1, "C", 2, 3, 4, "D", 5, 6, 7, 8, "M", 9, 10, 11, 12, 13, 14, 15]
-EXTRA = {
-    0: [("bias", 0)], 2: [("c3", 0)], 3: [("c3", 1)], 4: [("x", 0)],
-    5: [("D", 0)], 6: [("D", 1)], 7: [("D", 2)], 8: [("D", 3)],
-    9: [("M", 0)], 10: [("M", 1)], 11: [("M", 2)], 12: [("M", 3)],
-}
+RAW_BUFS = 8
 WARM = 6
-DUMMY_AFTER_BANK = {"A": [0, 1, 2, 3], 0: [1, 3], 1: [1, 3]}
-EW_GPSIMD_UNTIL = 0
-TANH_DELAY = 1
-MID_DELAY = 1
+HEAD_DUMMIES = 2
+CELL_ON_GPSIMD = False
+SMALL = [
+    ("bias", 0), None, ("c3", 0), ("x", 0), ("Wd", 0), ("Wm", 0), ("Wm", 1), ("Wd", 1),
+    ("Wm", 2), ("c3", 1), ("Wm", 3), ("Wd", 2), ("Wd", 3), None, None, None,
+]
 
 
 def tile_network_pb_kernel(
@@ -41,8 +34,9 @@ def tile_network_pb_kernel(
     with ExitStack() as ctx:
         const = ctx.enter_context(tc.tile_pool(name="const", bufs=1))
         rawp = ctx.enter_context(tc.tile_pool(name="rawp", bufs=RAW_BUFS))
+        srawp = ctx.enter_context(tc.tile_pool(name="srawp", bufs=4))
         grpp = ctx.enter_context(tc.tile_pool(name="grpp", bufs=3))
-        grpx = ctx.enter_context(tc.tile_pool(name="grpx", bufs=1))
+        sgrpp = ctx.enter_context(tc.tile_pool(name="sgrpp", bufs=2))
         codp = ctx.enter_context(tc.tile_pool(name="codp", bufs=4))
         gactp = ctx.enter_context(tc.tile_pool(name="gactp", bufs=2))
         ew1 = ctx.enter_context(tc.tile_pool(name="ew1", bufs=1))
@@ -54,80 +48,27 @@ def tile_network_pb_kernel(
         ctx.enter_context(tc.manual_schedule())
 
         ones = const.tile([P, P], BF16)
-        zz = const.tile([P, 512], BF16)
+        zeros = const.tile([P, 512], BF16)
         braw = const.tile([P, 256], BF16)
-        bmz = const.tile([P, 512], BF16)
-        dum = const.tile([P, 1], F32)
-        dum2 = const.tile([P, 1], F32)
+        bmrow = const.tile([P, 512], BF16)
+        tiny_in = const.tile([P, 1], F32)
+        tiny_out = const.tile([P, 1], F32)
         nc.vector.memset(ones[:], 1.0)
-        nc.vector.memset(zz[:], 0.0)
+        nc.vector.memset(zeros[:], 0.0)
         nc.vector.memset(braw[:], 0.0)
-        nc.vector.memset(bmz[:], 0.0)
-        nc.vector.memset(dum[:], 0.0)
+        nc.vector.memset(bmrow[:], 0.0)
+        nc.vector.memset(tiny_in[:], 0.0)
         nc.scalar.dma_start(out=braw[0:16, :], in_=bih3.rearrange("(r c) -> r c", c=256))
         nc.scalar.dma_start(out=braw[16:32, :], in_=bhh3.rearrange("(r c) -> r c", c=256))
         nc.scalar.dma_start(out=braw[32:36, :], in_=bd.rearrange("(r c) -> r c", c=256))
-        nc.scalar.dma_start(out=bmz[0:1, :], in_=bm.rearrange("(o m) -> o m", o=1))
-        nc.scalar.activation(out=dum2[:], in_=dum[:], func=AF.Sigmoid)
+        nc.scalar.dma_start(out=bmrow[0:1, :], in_=bm.rearrange("(o m) -> o m", o=1))
+        nc.scalar.activation(out=tiny_out[:], in_=tiny_in[:], func=AF.Sigmoid)
         ident = const.tile([P, P], F32)
         make_identity(nc, ident[:])
-
-        dmy = dpp.tile([P, 512], F32, tag="dp", name="dmy")
+        idle_bank = dpp.tile([P, 512], F32, tag="dp", name="idle_bank")
 
         def dummy():
-            nc.tensor.matmul(out=dmy[:], lhsT=ones[:], rhs=zz[:], start=True, stop=True)
-
-        wviews = [
-            w.rearrange("(g j p e) k -> g j p (e k)", g=4, j=4, p=P, e=2) for w in (Wih3, Whh3)
-        ]
-        raws = {}
-        released = set()
-        nloaded = [0]
-
-        def load_unit(key):
-            raw = rawp.tile([P, 4096], BF16, tag="raw", name="raw")
-            if key == "A":
-                for m, src in enumerate((y2, h3)):
-                    nc.sync.dma_start(
-                        out=raw[:, m * 2048 : (m + 1) * 2048].rearrange("p (t k) -> p t k", t=2),
-                        in_=src.rearrange("(t p) k -> p t k", p=P),
-                    )
-            elif key == "C":
-                nc.sync.dma_start(
-                    out=raw[:, 0:2048].rearrange("p (t k) -> p t k", t=2),
-                    in_=c3.rearrange("(t p) k -> p t k", p=P),
-                )
-                nc.sync.dma_start(
-                    out=raw[:, 2048:3072].rearrange("p (t k) -> p t k", t=2),
-                    in_=x.rearrange("(t p) k -> p t k", p=P),
-                )
-            elif key == "D":
-                nc.sync.dma_start(
-                    out=raw[:].rearrange("p (j f) -> p j f", j=4),
-                    in_=Wd.rearrange("(j p e) k -> p j (e k)", j=4, p=P, e=2),
-                )
-            elif key == "M":
-                nc.sync.dma_start(
-                    out=raw[:].rearrange("p (a k) -> p a k", a=4),
-                    in_=Wm.rearrange("(a p) k -> p a k", p=P),
-                )
-            else:
-                for m in range(2):
-                    nc.sync.dma_start(
-                        out=raw[:, m * 2048 : (m + 1) * 2048], in_=wviews[m][key % 4, key // 4]
-                    )
-            raws[key] = raw
-
-        def load_more():
-            while nloaded[0] < len(LOADS) and (
-                nloaded[0] < RAW_BUFS or LOADS[nloaded[0] - RAW_BUFS] in released
-            ):
-                load_unit(LOADS[nloaded[0]])
-                nloaded[0] += 1
-
-        load_more()
-        for i in range(WARM):
-            dummy()
+            nc.tensor.matmul(out=idle_bank[:], lhsT=ones[:], rhs=zeros[:], start=True, stop=True)
 
         acod = const.tile([P, 1024], U32, align_bytes=64)
         ascl = const.tile([P, 1024], U8, align_bytes=64)
@@ -135,37 +76,73 @@ def tile_network_pb_kernel(
         xscl = const.tile([P, 256], U8, align_bytes=64)
         dcod = const.tile([P, 1024], U32, align_bytes=64)
         dscl = const.tile([P, 1024], U8, align_bytes=64)
+        wmgrp = const.tile([P, 4096], BF16, align_bytes=64)
         wmcod = const.tile([P, 1024], U32, align_bytes=64)
         wmscl = const.tile([P, 1024], U8, align_bytes=64)
         mcod = const.tile([P, 512], U32, align_bytes=64)
         mscl = const.tile([P, 512], U8, align_bytes=64)
-        xgrp = const.tile([P, 1024], BF16, align_bytes=64)
         cT = const.tile([P, 4, 256], F32)
         bT = const.tile([P, 72], F32)
         bsum = const.tile([P, 32], F32)
         bmbc = const.tile([P, 512], F32)
         midT = const.tile([P, 2, 4, 256], BF16)
-        gm = const.tile([P, 2, 1024], BF16, align_bytes=64)
+        midgrp = const.tile([P, 2, 1024], BF16, align_bytes=64)
 
-        load = {"v": 0.0, "s": 0.0}
-        codes = {}
-        done = set()
-        big = {}
+        wviews = [
+            w.rearrange("(g j p e) k -> g j p (e k)", g=4, j=4, p=P, e=2) for w in (Wih3, Whh3)
+        ]
+        raws = {}
+        sraws = {}
 
-        def copy_out(out_ap, in_ap, eng=None):
-            if eng is None:
-                eng = "v" if load["v"] <= load["s"] else "s"
-            if eng == "v":
+        def load_acts():
+            raw = rawp.tile([P, 4096], BF16, tag="raw", name="raw")
+            for m, src in enumerate((y2, h3)):
+                nc.sync.dma_start(
+                    out=raw[:, m * 2048 : (m + 1) * 2048].rearrange("p (t k) -> p t k", t=2),
+                    in_=src.rearrange("(t p) k -> p t k", p=P),
+                )
+            raws["acts"] = raw
+
+        def load_unit(q):
+            if q >= UNITS:
+                return
+            job = SMALL[q]
+            if job is not None and job[0] != "bias":
+                kind, i = job
+                sraw = srawp.tile([P, 1024], BF16, tag="sraw", name="sraw")
+                two = sraw[:].rearrange("p (t k) -> p t k", t=2)
+                if kind == "c3":
+                    src = c3.rearrange("(t p) k -> p t k", p=P)[:, :, i * 512 : (i + 1) * 512]
+                    nc.sync.dma_start(out=two, in_=src)
+                elif kind == "x":
+                    nc.sync.dma_start(out=two, in_=x.rearrange("(t p) k -> p t k", p=P))
+                elif kind == "Wd":
+                    src = Wd.rearrange("(j p e) k -> j p (e k)", j=4, p=P, e=2)
+                    nc.sync.dma_start(out=sraw[:], in_=src[i])
+                else:
+                    nc.sync.dma_start(out=sraw[:], in_=Wm[i * P : (i + 1) * P, :])
+                sraws[q] = sraw
+            raw = rawp.tile([P, 4096], BF16, tag="raw", name="raw")
+            for m in range(2):
+                nc.sync.dma_start(
+                    out=raw[:, m * 2048 : (m + 1) * 2048], in_=wviews[m][q % 4, q // 4]
+                )
+            raws[q] = raw
+
+        def copy_out(on_vector, out_ap, in_ap):
+            if on_vector:
                 nc.vector.tensor_copy(out=out_ap, in_=in_ap)
             else:
                 nc.scalar.copy(out=out_ap, in_=in_ap)
-            load[eng] += 440.0
 
         def t_bank(srcs):
             tp = tpp.tile([P, 4, P], F32, tag="tp", name="tp")
-            for q, s in enumerate(srcs):
-                nc.tensor.transpose(tp[:, q, :], s, ident[:])
+            for n, s in enumerate(srcs):
+                nc.tensor.transpose(tp[:, n, :], s, ident[:])
             return tp
+
+        def four(words, w0):
+            return [words[:, w0 + n * P : w0 + (n + 1) * P] for n in range(4)]
 
         def pairs(tp):
             return tp[:].rearrange("w (a u) p -> w a p u", a=2, u=2)
@@ -173,109 +150,8 @@ def tile_network_pb_kernel(
         def pair_dst(ap):
             return ap.rearrange("w (a p u) -> w a p u", a=2, p=P, u=2)
 
-        def quant(cod_ap, scl_ap, in_ap, cols, flag=None):
+        def quant(cod_ap, scl_ap, in_ap):
             nc.vector.quantize_mx(out=cod_ap.bitcast(FP8X4), scales=scl_ap, in_=in_ap)
-            load["v"] += 12.0 + 0.22 * cols
-            if flag is not None:
-                done.add(flag)
-
-        def unit_T(u):
-            todo = []
-            rawf = raws[u][:].bitcast(F32)
-            grp = grpp.tile([P, 4096], BF16, tag="grp", name="grp", align_bytes=64)
-            grpf = grp[:].bitcast(F32)
-            dums = DUMMY_AFTER_BANK.get(u, [])
-            if u == "A":
-                for c in range(4):
-                    m, bt = c // 2, c % 2
-                    w0 = m * 1024 + bt * 512
-                    tp = t_bank([rawf[:, w0 + q * P : w0 + (q + 1) * P] for q in range(4)])
-                    dst = grpf[:, m * 1024 : (m + 1) * 1024].rearrange(
-                        "w (a b u) -> w a b u", a=2, b=B, u=2
-                    )
-                    copy_out(dst[:, :, bt * P : (bt + 1) * P, :], pairs(tp))
-                    if c in dums:
-                        dummy()
-                    if c == 2:
-                        quant(acod[:, 0:512], ascl[:, 0:512], grp[:, 0:2048], 2048)
-                todo.append(
-                    lambda: quant(acod[:, 512:1024], ascl[:, 512:1024], grp[:, 2048:4096], 2048)
-                )
-                return todo
-            cod = codp.tile([P, 1024], U32, tag="cod", name="cod", align_bytes=64)
-            scl = codp.tile([P, 1024], U8, tag="scl", name="scl", align_bytes=64)
-            codes[u] = (cod, scl)
-            order = [0, 2, 1, 3] if u == 0 else [0, 1, 2, 3]
-            for n, c in enumerate(order):
-                e, m = c // 2, c % 2
-                w0 = m * 1024 + e * 512
-                tp = t_bank([rawf[:, w0 + q * P : w0 + (q + 1) * P] for q in range(4)])
-                copy_out(pair_dst(grpf[:, c * 512 : (c + 1) * 512]), pairs(tp))
-                if n in dums:
-                    dummy()
-                if HALFQ and u != 0 and n == 2:
-                    quant(cod[:, 0:512], scl[:, 0:512], grp[:, 0:2048], 2048)
-            if HALFQ and u != 0:
-                todo.append(
-                    lambda: quant(cod[:, 512:1024], scl[:, 512:1024], grp[:, 2048:4096], 2048)
-                )
-            else:
-                todo.append(lambda: quant(cod[:], scl[:], grp[:], 4096))
-            return todo
-
-        def extra_bank(kind, i):
-            if kind == "bias":
-                tp = t_bank([braw[:].bitcast(F32)])
-                nc.vector.tensor_copy(out=bT[:], in_=tp[:].bitcast(BF16)[:, 0, 0:72])
-                nc.vector.tensor_tensor(out=bsum[:], in0=bT[:, 0:32], in1=bT[:, 32:64], op=ALU.add)
-                bmp = tpp.tile([P, 512], F32, tag="tp", name="bmp")
-                nc.tensor.matmul(out=bmp[:], lhsT=ones[:], rhs=bmz[:], start=True, stop=True)
-                copy_out(bmbc[:], bmp[:])
-                return []
-            if kind == "c3":
-                cf = raws["C"][:].bitcast(F32)
-                tp = t_bank(
-                    [
-                        cf[:, bt * 512 + (2 * i + jl) * P : bt * 512 + (2 * i + jl + 1) * P]
-                        for jl in range(2)
-                        for bt in range(2)
-                    ]
-                )
-                copy_out(
-                    cT[:, 2 * i : 2 * i + 2, :].rearrange("w a b -> w (a b)"),
-                    tp[:].rearrange("w q p -> w (q p)"),
-                )
-                done.add(("c3", i))
-                return []
-            if kind == "x":
-                cf = raws["C"][:].bitcast(F32)
-                tp = t_bank(
-                    [
-                        cf[:, 1024 + bt * 256 + uu * P : 1024 + bt * 256 + (uu + 1) * P]
-                        for bt in range(2)
-                        for uu in range(2)
-                    ]
-                )
-                copy_out(pair_dst(xgrp[:].bitcast(F32)), pairs(tp))
-                released.add("C")
-                return [lambda: quant(xcod[:], xscl[:], xgrp[:], 1024, "qx")]
-            rawf = raws[kind][:].bitcast(F32)
-            if i == 0:
-                big[kind] = grpx.tile([P, 4096], BF16, tag="big", name="big", align_bytes=64)
-            grp = big[kind]
-            grpf = grp[:].bitcast(F32)
-            tp = t_bank([rawf[:, i * 512 + q * P : i * 512 + (q + 1) * P] for q in range(4)])
-            if kind == "M":
-                dst = grpf.rearrange("w (a m u) -> w a m u", a=2, m=512, u=2)
-                copy_out(dst[:, :, i * P : (i + 1) * P, :], pairs(tp))
-            else:
-                copy_out(pair_dst(grpf[:, i * 512 : (i + 1) * 512]), pairs(tp))
-            if i < 3:
-                return []
-            released.add(kind)
-            if kind == "D":
-                return [lambda: quant(dcod[:], dscl[:], grp[:], 4096, "qD")]
-            return [lambda: quant(wmcod[:], wmscl[:], grp[:], 4096, "qM")]
 
         def mx(out_ap, l_cod, l_scl, l0, r_cod, r_scl, r0, n, start, stop):
             nc.tensor.matmul_mx(
@@ -288,7 +164,105 @@ def tile_network_pb_kernel(
                 stop=stop,
             )
 
-        def mx_group(out_ap, q, e):
+        grps = {}
+        codes = {}
+        gts = {}
+        gacts = {}
+        cell = {}
+        dps = {}
+        sgrps = {}
+
+        def acts_unit():
+            words = raws["acts"][:].bitcast(F32)
+            grp = grpp.tile([P, 4096], BF16, tag="grp", name="grp", align_bytes=64)
+            grpf = grp[:].bitcast(F32)
+            for c in range(4):
+                m, bt = c // 2, c % 2
+                tp = t_bank(four(words, c * 512))
+                dst = grpf[:, m * 1024 : (m + 1) * 1024].rearrange(
+                    "w (a b u) -> w a b u", a=2, b=B, u=2
+                )
+                copy_out(c % 2 == 0, dst[:, :, bt * P : (bt + 1) * P, :], pairs(tp))
+                dummy()
+                if c == 2:
+                    quant(acod[:, 0:512], ascl[:, 0:512], grp[:, 0:2048])
+            grps["acts"] = grp
+
+        def unit_transposes(q):
+            words = raws[q][:].bitcast(F32)
+            grp = grpp.tile([P, 4096], BF16, tag="grp", name="grp", align_bytes=64)
+            grpf = grp[:].bitcast(F32)
+            cod = codp.tile([P, 1024], U32, tag="cod", name="cod", align_bytes=64)
+            scl = codp.tile([P, 1024], U8, tag="scl", name="scl", align_bytes=64)
+            grps[q] = grp
+            codes[q] = (cod, scl)
+            for c in range(4):
+                e, m = c // 2, c % 2
+                tp = t_bank(four(words, m * 1024 + e * 512))
+                copy_out(c == 3 and q < UNITS - 1, pair_dst(grpf[:, c * 512 : (c + 1) * 512]), pairs(tp))
+                if q < HEAD_DUMMIES:
+                    dummy()
+                if c == 2:
+                    quant(cod[:, 0:512], scl[:, 0:512], grp[:, 0:2048])
+
+        def quant_rest(q):
+            if q == -1:
+                quant(acod[:, 512:1024], ascl[:, 512:1024], grps["acts"][:, 2048:4096])
+            elif 0 <= q < UNITS:
+                cod, scl = codes[q]
+                quant(cod[:, 512:1024], scl[:, 512:1024], grps[q][:, 2048:4096])
+
+        def small_bank(q):
+            job = SMALL[q]
+            if job is None:
+                return
+            kind, i = job
+            on_vector = False
+            if kind == "bias":
+                tp = t_bank([braw[:].bitcast(F32)])
+                nc.vector.tensor_copy(out=bT[:], in_=tp[:].bitcast(BF16)[:, 0, 0:72])
+                nc.vector.tensor_tensor(out=bsum[:], in0=bT[:, 0:32], in1=bT[:, 32:64], op=ALU.add)
+                bmp = tpp.tile([P, 512], F32, tag="tp", name="bmp")
+                nc.tensor.matmul(out=bmp[:], lhsT=ones[:], rhs=bmrow[:], start=True, stop=True)
+                copy_out(False, bmbc[:], bmp[:])
+                return
+            words = sraws[q][:].bitcast(F32)
+            if kind == "c3":
+                tp = t_bank(
+                    [
+                        words[:, bt * 256 + jl * P : bt * 256 + (jl + 1) * P]
+                        for jl in range(2)
+                        for bt in range(2)
+                    ]
+                )
+                copy_out(
+                    on_vector,
+                    cT[:, 2 * i : 2 * i + 2, :].rearrange("w a b -> w (a b)"),
+                    tp[:].rearrange("w n p -> w (n p)"),
+                )
+                return
+            tp = t_bank(four(words, 0))
+            if kind == "Wm":
+                dst = wmgrp[:].bitcast(F32).rearrange("w (a m u) -> w a m u", a=2, m=512, u=2)
+                copy_out(on_vector, dst[:, :, i * P : (i + 1) * P, :], pairs(tp))
+                return
+            sgrp = sgrpp.tile([P, 1024], BF16, tag="sgrp", name="sgrp", align_bytes=64)
+            copy_out(on_vector, pair_dst(sgrp[:].bitcast(F32)), pairs(tp))
+            sgrps[q] = sgrp
+
+        def small_quant(q):
+            job = SMALL[q] if q >= 0 else None
+            if job is None:
+                return
+            kind, i = job
+            if kind == "x":
+                quant(xcod[:], xscl[:], sgrps[q][:])
+            elif kind == "Wd":
+                quant(dcod[:, i * 256 : (i + 1) * 256], dscl[:, i * 256 : (i + 1) * 256], sgrps[q][:])
+            elif kind == "Wm" and i == 3:
+                quant(wmcod[:], wmscl[:], wmgrp[:])
+
+        def gate_group(out_ap, q, e):
             cod, scl = codes[q]
             for m in range(2):
                 for g in range(2):
@@ -298,249 +272,184 @@ def tile_network_pb_kernel(
                         (m == 0 and g == 0), (m == 1 and g == 1),
                     )
 
-        def mx_part(q):
+        def gate_passes(q):
+            if not 0 <= q < UNITS - 1:
+                return
             gt = gtp.tile([P, 2, B], F32, tag="gt", name="gt")
             for e in range(2):
-                mx_group(gt[:, e, :], q, e)
-            return gt
+                gate_group(gt[:, e, :], q, e)
+            gts[q] = gt
 
-        def d_pass(jj):
-            dt_ = dpp.tile([P, 2, B], F32, tag="dp", name="dpt")
+        def skip_passes(jj):
+            dp = dpp.tile([P, 2, B], F32, tag="dp", name="dp")
             for e in range(2):
-                mx(dt_[:, e, :], dcod, dscl, (2 * jj + e) * P, xcod, xscl, 0, B, True, True)
-            return dt_
+                mx(dp[:, e, :], dcod, dscl, (2 * jj + e) * P, xcod, xscl, 0, B, True, True)
+            dps[jj] = dp
 
-        st = {"gact": {}, "a": {}, "b": {}, "cn": {}, "tc": {}, "y": {}, "dp": {}}
-
-        def act_gate(q, e, in_ap):
+        def gate_function(q, e, in_ap):
             jj, gate = q // 4, q % 4
             col = (gate * 4 + jj) * 2 + e
             nc.scalar.activation(
-                out=st["gact"][jj][:, gate, e, :],
+                out=gacts[jj][:, gate, e, :],
                 in_=in_ap,
                 func=(AF.Tanh if gate == 2 else AF.Sigmoid),
                 bias=bsum[:, col : col + 1],
                 scale=1.0,
             )
-            load["s"] += 260.0
 
-        def act_part(q, gt):
+        def gate_functions(q):
+            if not 0 <= q < UNITS - 1:
+                return
             if q % 4 == 0:
-                st["gact"][q // 4] = gactp.tile([P, 4, 2, B], F32, tag="gact", name="gact")
+                gacts[q // 4] = gactp.tile([P, 4, 2, B], F32, tag="gact", name="gact")
             for e in range(2):
-                act_gate(q, e, gt[:, e, :])
+                gate_function(q, e, gts[q][:, e, :])
 
-        def ew_tt(jj, out_ap, in0, in1, op):
-            if jj < EW_GPSIMD_UNTIL:
+        def cell_tt(jj, out_ap, in0, in1, op):
+            if CELL_ON_GPSIMD and jj < 3:
                 nc.gpsimd.tensor_tensor(out=out_ap, in0=in0, in1=in1, op=op)
             else:
                 nc.vector.tensor_tensor(out=out_ap, in0=in0, in1=in1, op=op)
-                load["v"] += 480.0
 
-        def ew_a(jj):
-            a_t = ew1.tile([P, 2, B], F32, tag="a", name="a_t")
-            cv = cT[:].bitcast(BF16)[:, jj, :].rearrange("p (b e) -> p e b", e=2)
-            ew_tt(jj, a_t[:], st["gact"][jj][:, 1, :, :], cv, ALU.mult)
-            st["a"][jj] = a_t
+        def new_cell_tiles(jj):
+            cell[jj] = {
+                "fc": ew1.tile([P, 2, B], F32, tag="fc", name="fc"),
+                "ig": ew1.tile([P, 2, B], F32, tag="ig", name="ig"),
+                "th": ew1.tile([P, 2, B], F32, tag="th", name="th"),
+                "cn": ew4.tile([P, 2, B], F32, tag="cn", name="cn"),
+                "y": ew4.tile([P, 2, B], F32, tag="y", name="y"),
+            }
 
-        def ew_cn(jj):
-            b_t = ew1.tile([P, 2, B], F32, tag="b", name="b_t")
-            ga = st["gact"][jj]
-            ew_tt(jj, b_t[:], ga[:, 0, :, :], ga[:, 2, :, :], ALU.mult)
-            cn = ew4.tile([P, 2, B], F32, tag="cn", name="cn")
-            ew_tt(jj, cn[:], st["a"][jj][:], b_t[:], ALU.add)
-            st["cn"][jj] = cn
-
-        def act_tanh_c(jj):
-            tc_t = ew1.tile([P, 2, B], F32, tag="tc", name="tc_t")
-            nc.scalar.activation(out=tc_t[:], in_=st["cn"][jj][:], func=AF.Tanh)
-            load["s"] += 445.0
-            st["tc"][jj] = tc_t
-
-        def ew_y(jj):
-            y_t = ew4.tile([P, 2, B], F32, tag="y", name="y_t")
-            ew_tt(jj, y_t[:], st["gact"][jj][:, 3, :, :], st["tc"][jj][:], ALU.mult)
-            st["y"][jj] = y_t
-
-        def mid_half(jj, e):
+        def skip_sum(jj, e):
             nc.vector.scalar_tensor_tensor(
                 out=midT[:, jj // 2, 2 * (jj % 2) + e, :],
-                in0=st["dp"][jj][:, e, :],
+                in0=dps[jj][:, e, :],
                 scalar=bT[:, 64 + 2 * jj + e : 65 + 2 * jj + e],
-                in1=st["y"][jj][:, e, :],
+                in1=cell[jj]["y"][:, e, :],
                 op0=ALU.add,
                 op1=ALU.add,
             )
-            load["v"] += 270.0
 
         def mid_regroup(jj):
             g, uu = jj // 2, jj % 2
             nc.vector.tensor_copy(
-                out=gm[:, g, :].rearrange("p (b t) -> p b t", t=4)[:, :, 2 * uu : 2 * uu + 2],
+                out=midgrp[:, g, :].rearrange("p (b t) -> p b t", t=4)[:, :, 2 * uu : 2 * uu + 2],
                 in_=midT[:, g, 2 * uu : 2 * uu + 2, :].rearrange("p t b -> p b t"),
             )
-            load["v"] += 330.0
 
         def quant_mid(g):
-            quant(mcod[:, g * B : (g + 1) * B], mscl[:, g * B : (g + 1) * B], gm[:, g, :], 1024)
+            quant(mcod[:, g * B : (g + 1) * B], mscl[:, g * B : (g + 1) * B], midgrp[:, g, :])
 
-        def out_T(jj, bt):
+        def cell_work(q):
+            if not 0 <= q < UNITS - 2:
+                return
+            jj, gate = q // 4, q % 4
+            if gate == 0:
+                new_cell_tiles(jj)
+                if jj > 0:
+                    skip_sum(jj - 1, 0)
+                    skip_sum(jj - 1, 1)
+                    mid_regroup(jj - 1)
+                return
+            ga, t = gacts[jj], cell[jj]
+            if gate == 1:
+                if jj == 2:
+                    quant_mid(0)
+                cv = cT[:].bitcast(BF16)[:, jj, :].rearrange("p (b e) -> p e b", e=2)
+                cell_tt(jj, t["fc"][:], ga[:, 1, :, :], cv, ALU.mult)
+            elif gate == 2:
+                cell_tt(jj, t["ig"][:], ga[:, 0, :, :], ga[:, 2, :, :], ALU.mult)
+                cell_tt(jj, t["cn"][:], t["fc"][:], t["ig"][:], ALU.add)
+            else:
+                nc.scalar.activation(out=t["th"][:], in_=t["cn"][:], func=AF.Tanh)
+                cell_tt(jj, t["y"][:], ga[:, 3, :, :], t["th"][:], ALU.mult)
+
+        def out_transposes(jj, bt):
             ot = tpp.tile([P, 4, P], F32, tag="tp", name="ot")
-            for si, src in enumerate((st["y"][jj], st["cn"][jj])):
+            for si, key in enumerate(("y", "cn")):
                 for e in range(2):
                     nc.tensor.transpose(
-                        ot[:, si * 2 + e, :], src[:, e, bt * P : (bt + 1) * P], ident[:]
+                        ot[:, si * 2 + e, :], cell[jj][key][:, e, bt * P : (bt + 1) * P], ident[:]
                     )
             return (jj, bt, ot)
 
-        def out_store(item, eng):
+        def out_store(item, on_vector):
             jj, bt, ot = item
             res = resp.tile([P, 2, B], F32, tag="res", name="res")
             copy_out(
+                on_vector,
                 res[:].rearrange("b s (p e) -> b s p e", e=2),
                 ot[:].rearrange("b (s e) p -> b s p e", s=2, e=2),
-                eng,
             )
             rows = slice(bt * P, (bt + 1) * P)
             cols = slice(jj * B, (jj + 1) * B)
             nc.sync.dma_start(out=out_1[rows, cols], in_=res[:, 0, :])
             nc.sync.dma_start(out=out_2[rows, cols], in_=res[:, 1, :])
 
-        pos = {}
-        for i, u in enumerate(TUNITS):
-            pos[u] = i
-        pend_q = []
-        pend_part = []
-        due = {}
-        next_part = 0
-        step = -1
-        while step < len(TUNITS) - 1 or ("mid", 2) not in done or "qmid0" not in done:
-            step += 1
-            u = TUNITS[step] if step < len(TUNITS) else None
-            for q, gt in pend_part:
-                act_part(q, gt)
-                done.add(("act", q))
-            pend_part = []
-            for jj in range(3):
-                if due.get(("tanh", jj), 99) <= step and ("tanh", jj) not in done:
-                    act_tanh_c(jj)
-                    done.add(("tanh", jj))
-            for f in pend_q:
-                f()
-            pend_q = []
-            if due.get("qmid0", 99) <= step and "qmid0" not in done:
-                quant_mid(0)
-                done.add("qmid0")
-            for jj in range(3):
-                if due.get(("mid", jj), 99) <= step and ("mid", jj) not in done and jj in st["dp"]:
-                    mid_half(jj, 0)
-                    mid_half(jj, 1)
-                    mid_regroup(jj)
-                    done.add(("mid", jj))
-                    if jj == 1:
-                        due["qmid0"] = step + 1
-            for jj in range(4):
-                if (
-                    ("act", 4 * jj + 1) in done
-                    and ("c3", jj // 2) in done
-                    and ("A", jj) not in done
-                ):
-                    ew_a(jj)
-                    done.add(("A", jj))
-                if jj == 3:
-                    continue
-                if ("act", 4 * jj + 2) in done and ("A", jj) in done and ("cn", jj) not in done:
-                    ew_cn(jj)
-                    done.add(("cn", jj))
-                    due[("tanh", jj)] = step + TANH_DELAY
-                if ("tanh", jj) in done and ("act", 4 * jj + 3) in done and ("y", jj) not in done:
-                    ew_y(jj)
-                    done.add(("y", jj))
-                    due[("mid", jj)] = step + MID_DELAY
-            if u is not None:
-                pend_q = unit_T(u)
-                released.add(u)
-                for kind, i in EXTRA.get(u, []):
-                    pend_q = pend_q + extra_bank(kind, i)
-                load_more()
-            while (
-                next_part < 15
-                and len(pend_part) < 2
-                and pos[next_part] + (LAG if next_part < LAG1_FROM else 1) <= step
-            ):
-                pend_part.append((next_part, mx_part(next_part)))
-                next_part += 1
-            for jj in range(4):
-                if (
-                    jj not in st["dp"]
-                    and "qD" in done
-                    and "qx" in done
-                    and next_part > 4 * jj + 2
-                    and (jj == 0 or ("mid", jj - 1) in done)
-                ):
-                    st["dp"][jj] = d_pass(jj)
+        load_acts()
+        for q in range(RAW_BUFS - 1):
+            load_unit(q)
+        for n in range(WARM):
+            dummy()
+        acts_unit()
+        load_unit(RAW_BUFS - 1)
+        for s in range(UNITS):
+            gate_functions(s - 3)
+            quant_rest(s - 1)
+            small_quant(s - 1)
+            cell_work(s - 3)
+            unit_transposes(s)
+            small_bank(s)
+            load_unit(s + RAW_BUFS)
+            gate_passes(s - 2)
+            if s % 4 == 2 and s > 2:
+                skip_passes(s // 4 - 1)
 
-        for f in pend_q:
-            f()
-        while pend_part or next_part < 15:
-            for q, gt in pend_part:
-                act_part(q, gt)
-                if q == 13:
-                    ew_a(3)
-            pend_part = []
-            if next_part < 15:
-                pend_part.append((next_part, mx_part(next_part)))
-                next_part += 1
-        for jj in range(3):
-            assert ("mid", jj) in done
-        assert "qmid0" in done and "qM" in done
-        if 3 not in st["dp"]:
-            st["dp"][3] = d_pass(3)
+        quant_rest(15)
+        gate_functions(13)
+        cell_work(13)
+        gate_passes(14)
+        gate_functions(14)
+        skip_passes(3)
         o_banks = []
         for e in range(2):
             ob = tpp.tile([P, B], F32, tag="tp", name="ob")
-            mx_group(ob[:], 15, e)
+            gate_group(ob[:], 15, e)
             o_banks.append(ob)
-        ga = st["gact"][3]
-        b_t = ew1.tile([P, 2, B], F32, tag="b", name="b_t")
-        cn = ew4.tile([P, 2, B], F32, tag="cn", name="cn")
-        tc_t = ew1.tile([P, 2, B], F32, tag="tc", name="tc_t")
-        y_t = ew4.tile([P, 2, B], F32, tag="y", name="y_t")
-        st["cn"][3] = cn
-        st["y"][3] = y_t
+        ga, t = gacts[3], cell[3]
         for e in range(2):
             nc.vector.tensor_tensor(
-                out=b_t[:, e, :], in0=ga[:, 0, e, :], in1=ga[:, 2, e, :], op=ALU.mult
+                out=t["ig"][:, e, :], in0=ga[:, 0, e, :], in1=ga[:, 2, e, :], op=ALU.mult
             )
             nc.vector.tensor_tensor(
-                out=cn[:, e, :], in0=st["a"][3][:, e, :], in1=b_t[:, e, :], op=ALU.add
+                out=t["cn"][:, e, :], in0=t["fc"][:, e, :], in1=t["ig"][:, e, :], op=ALU.add
             )
         for e in range(2):
-            act_gate(15, e, o_banks[e][:])
-            nc.scalar.activation(out=tc_t[:, e, :], in_=cn[:, e, :], func=AF.Tanh)
+            gate_function(15, e, o_banks[e][:])
+            nc.scalar.activation(out=t["th"][:, e, :], in_=t["cn"][:, e, :], func=AF.Tanh)
         mps = []
         for bt in range(2):
             mp = gtp.tile([P, 512], F32, tag="gt", name="mp")
             mx(mp[:], mcod, mscl, bt * P, wmcod, wmscl, 0, 512, True, False)
             mps.append(mp)
         outs = [(jj, bt) for jj in range(4) for bt in range(2)]
-        banks = [out_T(jj, bt) for jj, bt in outs[0:3]]
+        banks = [out_transposes(jj, bt) for jj, bt in outs[0:3]]
         for e in range(2):
             nc.vector.tensor_tensor(
-                out=y_t[:, e, :], in0=ga[:, 3, e, :], in1=tc_t[:, e, :], op=ALU.mult
+                out=t["y"][:, e, :], in0=ga[:, 3, e, :], in1=t["th"][:, e, :], op=ALU.mult
             )
-            mid_half(3, e)
+            skip_sum(3, e)
         mid_regroup(3)
         quant_mid(1)
         for item in banks:
-            out_store(item, "s")
-        banks = [out_T(jj, bt) for jj, bt in outs[3:5]]
-        out_store(banks[0], "s")
-        nc.scalar.activation(out=dum2[:], in_=dum[:], func=AF.Exp)
+            out_store(item, False)
+        banks = [out_transposes(jj, bt) for jj, bt in outs[3:5]]
+        out_store(banks[0], False)
+        nc.scalar.activation(out=tiny_out[:], in_=tiny_in[:], func=AF.Exp)
         for bt in range(2):
             mx(mps[bt][:], mcod, mscl, B + bt * P, wmcod, wmscl, 512, 512, False, True)
-        out_store(banks[1], "v")
-        banks = [out_T(jj, bt) for jj, bt in outs[5:8]]
+        out_store(banks[1], True)
+        banks = [out_transposes(jj, bt) for jj, bt in outs[5:8]]
         ssum = const.tile([P, 2], F32)
         lsum = const.tile([P, 2], F32)
         ex = const.tile([P, 512], F32)
@@ -559,7 +468,7 @@ def tile_network_pb_kernel(
             nmxs.append(nmx)
         nc.scalar.activation(out=lsum[:], in_=ssum[:], func=AF.Ln)
         for item in banks:
-            out_store(item, "v")
+            out_store(item, True)
         for bt in range(2):
             nc.vector.tensor_scalar(
                 out=mots[bt][:], in0=mots[bt][:], scalar1=nmxs[bt][:, 0:1],

@@ -18,8 +18,7 @@ UNITS = 16
 FLOPS = 2 * 256 * (4096 * 2048 + 1024 * 512 + 512 * 1024)
 
 RAW_BUFS = 8
-WARM = 6
-HEAD_DUMMIES = 2
+LAG = 2
 CELL_ON_GPSIMD = False
 SMALL = [
     ("bias", 0), None, ("c3", 0), ("x", 0), ("Wd", 0), ("Wm", 0), ("Wm", 1), ("Wd", 1),
@@ -48,13 +47,11 @@ def tile_network_pb_kernel(
         ctx.enter_context(tc.manual_schedule())
 
         ones = const.tile([P, P], BF16)
-        zeros = const.tile([P, 512], BF16)
         braw = const.tile([P, 256], BF16)
         bmrow = const.tile([P, 512], BF16)
         tiny_in = const.tile([P, 1], F32)
         tiny_out = const.tile([P, 1], F32)
         nc.vector.memset(ones[:], 1.0)
-        nc.vector.memset(zeros[:], 0.0)
         nc.vector.memset(braw[:], 0.0)
         nc.vector.memset(bmrow[:], 0.0)
         nc.vector.memset(tiny_in[:], 0.0)
@@ -65,10 +62,6 @@ def tile_network_pb_kernel(
         nc.scalar.activation(out=tiny_out[:], in_=tiny_in[:], func=AF.Sigmoid)
         ident = const.tile([P, P], F32)
         make_identity(nc, ident[:])
-        idle_bank = dpp.tile([P, 512], F32, tag="dp", name="idle_bank")
-
-        def dummy():
-            nc.tensor.matmul(out=idle_bank[:], lhsT=ones[:], rhs=zeros[:], start=True, stop=True)
 
         acod = const.tile([P, 1024], U32, align_bytes=64)
         ascl = const.tile([P, 1024], U8, align_bytes=64)
@@ -183,7 +176,6 @@ def tile_network_pb_kernel(
                     "w (a b u) -> w a b u", a=2, b=B, u=2
                 )
                 copy_out(c % 2 == 0, dst[:, :, bt * P : (bt + 1) * P, :], pairs(tp))
-                dummy()
                 if c == 2:
                     quant(acod[:, 0:512], ascl[:, 0:512], grp[:, 0:2048])
             grps["acts"] = grp
@@ -200,8 +192,6 @@ def tile_network_pb_kernel(
                 e, m = c // 2, c % 2
                 tp = t_bank(four(words, m * 1024 + e * 512))
                 copy_out(c == 3 and q < UNITS - 1, pair_dst(grpf[:, c * 512 : (c + 1) * 512]), pairs(tp))
-                if q < HEAD_DUMMIES:
-                    dummy()
                 if c == 2:
                     quant(cod[:, 0:512], scl[:, 0:512], grp[:, 0:2048])
 
@@ -389,27 +379,25 @@ def tile_network_pb_kernel(
         load_acts()
         for q in range(RAW_BUFS - 1):
             load_unit(q)
-        for n in range(WARM):
-            dummy()
         acts_unit()
         load_unit(RAW_BUFS - 1)
         for s in range(UNITS):
-            gate_functions(s - 3)
+            gate_functions(s - LAG - 1)
             quant_rest(s - 1)
             small_quant(s - 1)
-            cell_work(s - 3)
+            cell_work(s - LAG - 1)
             unit_transposes(s)
             small_bank(s)
             load_unit(s + RAW_BUFS)
-            gate_passes(s - 2)
-            if s % 4 == 2 and s > 2:
-                skip_passes(s // 4 - 1)
+            gate_passes(s - LAG)
+            if (s - LAG) % 4 == 0 and s - LAG >= 4:
+                skip_passes((s - LAG) // 4 - 1)
 
-        quant_rest(15)
-        gate_functions(13)
-        cell_work(13)
-        gate_passes(14)
-        gate_functions(14)
+        quant_rest(UNITS - 1)
+        for q in range(UNITS - LAG - 1, UNITS - 1):
+            gate_functions(q)
+            cell_work(q)
+            gate_passes(q + 1)
         skip_passes(3)
         o_banks = []
         for e in range(2):

@@ -18,7 +18,7 @@ UNITS = 16
 FLOPS = 2 * 256 * (4096 * 2048 + 1024 * 512 + 512 * 1024)
 
 RAW_BUFS = 8
-LAG = 2
+LAG = 1
 CELL_ON_GPSIMD = False
 SMALL = [
     ("bias", 0), None, ("c3", 0), ("x", 0), ("Wd", 0), ("Wm", 0), ("Wm", 1), ("Wd", 1),
@@ -191,7 +191,7 @@ def tile_network_pb_kernel(
             for c in range(4):
                 e, m = c // 2, c % 2
                 tp = t_bank(four(words, m * 1024 + e * 512))
-                copy_out(c == 3 and q < UNITS - 1, pair_dst(grpf[:, c * 512 : (c + 1) * 512]), pairs(tp))
+                copy_out(c == 2, pair_dst(grpf[:, c * 512 : (c + 1) * 512]), pairs(tp))
                 if c == 2:
                     quant(cod[:, 0:512], scl[:, 0:512], grp[:, 0:2048])
 
@@ -339,7 +339,6 @@ def tile_network_pb_kernel(
                 if jj > 0:
                     skip_sum(jj - 1, 0)
                     skip_sum(jj - 1, 1)
-                    mid_regroup(jj - 1)
                 return
             ga, t = gacts[jj], cell[jj]
             if gate == 1:
@@ -349,10 +348,19 @@ def tile_network_pb_kernel(
                 cell_tt(jj, t["fc"][:], ga[:, 1, :, :], cv, ALU.mult)
             elif gate == 2:
                 cell_tt(jj, t["ig"][:], ga[:, 0, :, :], ga[:, 2, :, :], ALU.mult)
-                cell_tt(jj, t["cn"][:], t["fc"][:], t["ig"][:], ALU.add)
             else:
                 nc.scalar.activation(out=t["th"][:], in_=t["cn"][:], func=AF.Tanh)
                 cell_tt(jj, t["y"][:], ga[:, 3, :, :], t["th"][:], ALU.mult)
+
+        def cell_work_late(q):
+            if not 0 <= q < UNITS - 2:
+                return
+            jj, gate = q // 4, q % 4
+            if gate == 0 and jj > 0:
+                mid_regroup(jj - 1)
+            elif gate == 2:
+                t = cell[jj]
+                cell_tt(jj, t["cn"][:], t["fc"][:], t["ig"][:], ALU.add)
 
         def out_transposes(jj, bt):
             ot = tpp.tile([P, 4, P], F32, tag="tp", name="ot")
@@ -388,6 +396,7 @@ def tile_network_pb_kernel(
             cell_work(s - LAG - 1)
             unit_transposes(s)
             small_bank(s)
+            cell_work_late(s - LAG - 1)
             load_unit(s + RAW_BUFS)
             gate_passes(s - LAG)
             if (s - LAG) % 4 == 0 and s - LAG >= 4:
@@ -397,6 +406,7 @@ def tile_network_pb_kernel(
         for q in range(UNITS - LAG - 1, UNITS - 1):
             gate_functions(q)
             cell_work(q)
+            cell_work_late(q)
             gate_passes(q + 1)
         skip_passes(3)
         o_banks = []
@@ -409,6 +419,7 @@ def tile_network_pb_kernel(
             nc.vector.tensor_tensor(
                 out=t["ig"][:, e, :], in0=ga[:, 0, e, :], in1=ga[:, 2, e, :], op=ALU.mult
             )
+        for e in range(2):
             nc.vector.tensor_tensor(
                 out=t["cn"][:, e, :], in0=t["fc"][:, e, :], in1=t["ig"][:, e, :], op=ALU.add
             )
@@ -426,6 +437,7 @@ def tile_network_pb_kernel(
             nc.vector.tensor_tensor(
                 out=t["y"][:, e, :], in0=ga[:, 3, e, :], in1=t["th"][:, e, :], op=ALU.mult
             )
+        for e in range(2):
             skip_sum(3, e)
         mid_regroup(3)
         quant_mid(1)
@@ -445,14 +457,17 @@ def tile_network_pb_kernel(
         nmxs = []
         for bt in range(2):
             mot = const.tile([P, 512], F32, name="mot%d" % bt)
-            nmx = const.tile([P, 1], F32, name="nmx%d" % bt)
             nc.vector.tensor_tensor(out=mot[:], in0=mps[bt][:], in1=bmbc[:], op=ALU.add)
-            nc.vector.tensor_reduce(out=nmx[:], in_=mot[:], axis=AX.X, op=ALU.max, negate=True)
+            mots.append(mot)
+        for bt in range(2):
+            nmx = const.tile([P, 1], F32, name="nmx%d" % bt)
+            nc.vector.tensor_reduce(
+                out=nmx[:], in_=mots[bt][:], axis=AX.X, op=ALU.max, negate=True
+            )
             nc.scalar.activation(
-                out=ex[:], in_=mot[:], func=AF.Exp, bias=nmx[:, 0:1], scale=1.0,
+                out=ex[:], in_=mots[bt][:], func=AF.Exp, bias=nmx[:, 0:1], scale=1.0,
                 accum_out=ssum[:, bt : bt + 1],
             )
-            mots.append(mot)
             nmxs.append(nmx)
         nc.scalar.activation(out=lsum[:], in_=ssum[:], func=AF.Ln)
         for item in banks:

@@ -21,8 +21,8 @@ RAW_BUFS = 8
 LAG = 1
 CELL_ON_GPSIMD = False
 SMALL = [
-    ("bias", 0), None, ("c3", 0), ("x", 0), ("Wd", 0), ("Wm", 0), ("Wm", 1), ("Wd", 1),
-    ("Wm", 2), ("c3", 1), ("Wm", 3), ("Wd", 2), ("Wd", 3), None, None, None,
+    ("bias", 0), None, ("c3", 0), ("x", 0), ("Wd", 0), None, None, ("Wd", 1),
+    None, ("c3", 1), None, ("Wd", 2), None, ("Wd", 3), None, None,
 ]
 
 
@@ -41,9 +41,8 @@ def tile_network_pb_kernel(
         ew1 = ctx.enter_context(tc.tile_pool(name="ew1", bufs=1))
         ew4 = ctx.enter_context(tc.tile_pool(name="ew4", bufs=4))
         resp = ctx.enter_context(tc.tile_pool(name="resp", bufs=8))
-        tpp = ctx.enter_context(tc.psum_pool(name="tpp", bufs=5))
+        tpp = ctx.enter_context(tc.psum_pool(name="tpp", bufs=6))
         gtp = ctx.enter_context(tc.psum_pool(name="gtp", bufs=2))
-        dpp = ctx.enter_context(tc.psum_pool(name="dpp", bufs=1))
         ctx.enter_context(tc.manual_schedule())
 
         ones = const.tile([P, P], BF16)
@@ -69,6 +68,7 @@ def tile_network_pb_kernel(
         xscl = const.tile([P, 256], U8, align_bytes=64)
         dcod = const.tile([P, 1024], U32, align_bytes=64)
         dscl = const.tile([P, 1024], U8, align_bytes=64)
+        wmraw = const.tile([P, 4096], BF16)
         wmgrp = const.tile([P, 4096], BF16, align_bytes=64)
         wmcod = const.tile([P, 1024], U32, align_bytes=64)
         wmscl = const.tile([P, 1024], U8, align_bytes=64)
@@ -90,10 +90,11 @@ def tile_network_pb_kernel(
         def load_acts():
             raw = rawp.tile([P, 4096], BF16, tag="raw", name="raw")
             for m, src in enumerate((y2, h3)):
-                nc.sync.dma_start(
-                    out=raw[:, m * 2048 : (m + 1) * 2048].rearrange("p (t k) -> p t k", t=2),
-                    in_=src.rearrange("(t p) k -> p t k", p=P),
-                )
+                for t in range(2):
+                    c0 = (2 * m + t) * 1024
+                    nc.sync.dma_start(
+                        out=raw[:, c0 : c0 + 1024], in_=src[t * P : (t + 1) * P, :]
+                    )
             raws["acts"] = raw
 
         def load_unit(q):
@@ -109,11 +110,9 @@ def tile_network_pb_kernel(
                     nc.sync.dma_start(out=two, in_=src)
                 elif kind == "x":
                     nc.sync.dma_start(out=two, in_=x.rearrange("(t p) k -> p t k", p=P))
-                elif kind == "Wd":
+                else:
                     src = Wd.rearrange("(j p e) k -> j p (e k)", j=4, p=P, e=2)
                     nc.sync.dma_start(out=sraw[:], in_=src[i])
-                else:
-                    nc.sync.dma_start(out=sraw[:], in_=Wm[i * P : (i + 1) * P, :])
                 sraws[q] = sraw
             raw = rawp.tile([P, 4096], BF16, tag="raw", name="raw")
             for m in range(2):
@@ -232,10 +231,6 @@ def tile_network_pb_kernel(
                 )
                 return
             tp = t_bank(four(words, 0))
-            if kind == "Wm":
-                dst = wmgrp[:].bitcast(F32).rearrange("w (a m u) -> w a m u", a=2, m=512, u=2)
-                copy_out(on_vector, dst[:, :, i * P : (i + 1) * P, :], pairs(tp))
-                return
             sgrp = sgrpp.tile([P, 1024], BF16, tag="sgrp", name="sgrp", align_bytes=64)
             copy_out(on_vector, pair_dst(sgrp[:].bitcast(F32)), pairs(tp))
             sgrps[q] = sgrp
@@ -249,8 +244,24 @@ def tile_network_pb_kernel(
                 quant(xcod[:], xscl[:], sgrps[q][:])
             elif kind == "Wd":
                 quant(dcod[:, i * 256 : (i + 1) * 256], dscl[:, i * 256 : (i + 1) * 256], sgrps[q][:])
-            elif kind == "Wm" and i == 3:
-                quant(wmcod[:], wmscl[:], wmgrp[:])
+
+        def wm_bank(b):
+            a, h = b // 2, b % 2
+            words = wmraw[:].bitcast(F32)
+            return t_bank(
+                [
+                    words[:, i * 512 + (2 * a + u) * P : i * 512 + (2 * a + u + 1) * P]
+                    for i in (2 * h, 2 * h + 1)
+                    for u in range(2)
+                ]
+            )
+
+        def wm_copy(b, tp):
+            copy_out(False, pair_dst(wmgrp[:].bitcast(F32)[:, b * 512 : (b + 1) * 512]), pairs(tp))
+
+        def wm_quant(a):
+            half = slice(a * 512, (a + 1) * 512)
+            quant(wmcod[:, half], wmscl[:, half], wmgrp[:, a * 2048 : (a + 1) * 2048])
 
         def gate_group(out_ap, q, e):
             cod, scl = codes[q]
@@ -271,7 +282,7 @@ def tile_network_pb_kernel(
             gts[q] = gt
 
         def skip_passes(jj):
-            dp = dpp.tile([P, 2, B], F32, tag="dp", name="dp")
+            dp = gtp.tile([P, 2, B], F32, tag="gt", name="dp")
             for e in range(2):
                 mx(dp[:, e, :], dcod, dscl, (2 * jj + e) * P, xcod, xscl, 0, B, True, True)
             dps[jj] = dp
@@ -398,22 +409,30 @@ def tile_network_pb_kernel(
             small_bank(s)
             cell_work_late(s - LAG - 1)
             load_unit(s + RAW_BUFS)
+            if UNITS - 4 > s >= UNITS - 8:
+                i = s - (UNITS - 8)
+                nc.sync.dma_start(
+                    out=wmraw[:, i * 1024 : (i + 1) * 1024], in_=Wm[i * P : (i + 1) * P, :]
+                )
             gate_passes(s - LAG)
             if (s - LAG) % 4 == 0 and s - LAG >= 4:
                 skip_passes((s - LAG) // 4 - 1)
 
+        wm_banks = [wm_bank(b) for b in range(2)]
         quant_rest(UNITS - 1)
         for q in range(UNITS - LAG - 1, UNITS - 1):
             gate_functions(q)
             cell_work(q)
             cell_work_late(q)
             gate_passes(q + 1)
-        skip_passes(3)
+        wm_copy(0, wm_banks[0])
         o_banks = []
         for e in range(2):
             ob = tpp.tile([P, B], F32, tag="tp", name="ob")
             gate_group(ob[:], 15, e)
             o_banks.append(ob)
+        skip_passes(3)
+        wm_banks += [wm_bank(b) for b in range(2, 4)]
         ga, t = gacts[3], cell[3]
         for e in range(2):
             nc.vector.tensor_tensor(
@@ -426,11 +445,8 @@ def tile_network_pb_kernel(
         for e in range(2):
             gate_function(15, e, o_banks[e][:])
             nc.scalar.activation(out=t["th"][:, e, :], in_=t["cn"][:, e, :], func=AF.Tanh)
-        mps = []
-        for bt in range(2):
-            mp = gtp.tile([P, 512], F32, tag="gt", name="mp")
-            mx(mp[:], mcod, mscl, bt * P, wmcod, wmscl, 0, 512, True, False)
-            mps.append(mp)
+        for b in range(1, 4):
+            wm_copy(b, wm_banks[b])
         outs = [(jj, bt) for jj in range(4) for bt in range(2)]
         banks = [out_transposes(jj, bt) for jj, bt in outs[0:3]]
         for e in range(2):
@@ -439,8 +455,15 @@ def tile_network_pb_kernel(
             )
         for e in range(2):
             skip_sum(3, e)
+        wm_quant(0)
         mid_regroup(3)
+        wm_quant(1)
         quant_mid(1)
+        mps = []
+        for bt in range(2):
+            mp = gtp.tile([P, 512], F32, tag="gt", name="mp")
+            mx(mp[:], mcod, mscl, bt * P, wmcod, wmscl, 0, 512, True, False)
+            mps.append(mp)
         for item in banks:
             out_store(item, False)
         banks = [out_transposes(jj, bt) for jj, bt in outs[3:5]]

@@ -20,6 +20,8 @@ FLOPS = 2 * 256 * (4096 * 2048 + 1024 * 512 + 512 * 1024)
 RAW_BUFS = 8
 LAG = 1
 CELL_ON_GPSIMD = False
+LAST_PARTS = [[(0, 0), (2, 0)], [(1, 0), (0, 1)], [(2, 1), (1, 1)], [(3, 0), (3, 1)]]
+LAST_LOADS = [0, 2, 1, 3]
 SMALL = [
     ("bias", 0), None, ("c3", 0), ("x", 0), ("Wd", 0), None, None, ("Wd", 1),
     None, ("c3", 1), None, ("Wd", 2), None, ("Wd", 3), None, None,
@@ -41,8 +43,8 @@ def tile_network_pb_kernel(
         ew1 = ctx.enter_context(tc.tile_pool(name="ew1", bufs=1))
         ew4 = ctx.enter_context(tc.tile_pool(name="ew4", bufs=4))
         resp = ctx.enter_context(tc.tile_pool(name="resp", bufs=8))
-        tpp = ctx.enter_context(tc.psum_pool(name="tpp", bufs=6))
-        gtp = ctx.enter_context(tc.psum_pool(name="gtp", bufs=2))
+        tpp = ctx.enter_context(tc.psum_pool(name="tpp", bufs=5))
+        gtp = ctx.enter_context(tc.psum_pool(name="gtp", bufs=3))
         ctx.enter_context(tc.manual_schedule())
 
         ones = const.tile([P, P], BF16)
@@ -59,27 +61,27 @@ def tile_network_pb_kernel(
         nc.scalar.dma_start(out=braw[32:36, :], in_=bd.rearrange("(r c) -> r c", c=256))
         nc.scalar.dma_start(out=bmrow[0:1, :], in_=bm.rearrange("(o m) -> o m", o=1))
         nc.scalar.activation(out=tiny_out[:], in_=tiny_in[:], func=AF.Sigmoid)
-        ident = const.tile([P, P], F32)
+        ident = const.tile([P, P], F32, align_bytes=256)
         make_identity(nc, ident[:])
 
-        acod = const.tile([P, 1024], U32, align_bytes=64)
-        ascl = const.tile([P, 1024], U8, align_bytes=64)
-        xcod = const.tile([P, 256], U32, align_bytes=64)
-        xscl = const.tile([P, 256], U8, align_bytes=64)
-        dcod = const.tile([P, 1024], U32, align_bytes=64)
-        dscl = const.tile([P, 1024], U8, align_bytes=64)
-        wmraw = const.tile([P, 4096], BF16)
-        wmgrp = const.tile([P, 4096], BF16, align_bytes=64)
-        wmcod = const.tile([P, 1024], U32, align_bytes=64)
-        wmscl = const.tile([P, 1024], U8, align_bytes=64)
-        mcod = const.tile([P, 512], U32, align_bytes=64)
-        mscl = const.tile([P, 512], U8, align_bytes=64)
+        acod = const.tile([P, 1024], U32, align_bytes=256)
+        ascl = const.tile([P, 1024], U8, align_bytes=256)
+        xcod = const.tile([P, 256], U32, align_bytes=256)
+        xscl = const.tile([P, 256], U8, align_bytes=256)
+        dcod = const.tile([P, 1024], U32, align_bytes=256)
+        dscl = const.tile([P, 1024], U8, align_bytes=256)
+        wmraw = const.tile([P, 4096], BF16, align_bytes=256)
+        wmgrp = const.tile([P, 4096], BF16, align_bytes=256)
+        wmcod = const.tile([P, 1024], U32, align_bytes=256)
+        wmscl = const.tile([P, 1024], U8, align_bytes=256)
+        mcod = const.tile([P, 512], U32, align_bytes=256)
+        mscl = const.tile([P, 512], U8, align_bytes=256)
         cT = const.tile([P, 4, 256], F32)
         bT = const.tile([P, 72], F32)
         bsum = const.tile([P, 32], F32)
         bmbc = const.tile([P, 512], F32)
         midT = const.tile([P, 2, 4, 256], BF16)
-        midgrp = const.tile([P, 2, 1024], BF16, align_bytes=64)
+        midgrp = const.tile([P, 2, 1024], BF16, align_bytes=256)
 
         wviews = [
             w.rearrange("(g j p e) k -> g j p (e k)", g=4, j=4, p=P, e=2) for w in (Wih3, Whh3)
@@ -88,7 +90,7 @@ def tile_network_pb_kernel(
         sraws = {}
 
         def load_acts():
-            raw = rawp.tile([P, 4096], BF16, tag="raw", name="raw")
+            raw = rawp.tile([P, 4096], BF16, tag="raw", name="raw", align_bytes=256)
             for m, src in enumerate((y2, h3)):
                 for t in range(2):
                     c0 = (2 * m + t) * 1024
@@ -103,7 +105,7 @@ def tile_network_pb_kernel(
             job = SMALL[q]
             if job is not None and job[0] != "bias":
                 kind, i = job
-                sraw = srawp.tile([P, 1024], BF16, tag="sraw", name="sraw")
+                sraw = srawp.tile([P, 1024], BF16, tag="sraw", name="sraw", align_bytes=256)
                 two = sraw[:].rearrange("p (t k) -> p t k", t=2)
                 if kind == "c3":
                     src = c3.rearrange("(t p) k -> p t k", p=P)[:, :, i * 512 : (i + 1) * 512]
@@ -114,12 +116,16 @@ def tile_network_pb_kernel(
                     src = Wd.rearrange("(j p e) k -> j p (e k)", j=4, p=P, e=2)
                     nc.sync.dma_start(out=sraw[:], in_=src[i])
                 sraws[q] = sraw
-            raw = rawp.tile([P, 4096], BF16, tag="raw", name="raw")
+            raw = rawp.tile([P, 4096], BF16, tag="raw", name="raw", align_bytes=256)
             for m in range(2):
                 nc.sync.dma_start(
-                    out=raw[:, m * 2048 : (m + 1) * 2048], in_=wviews[m][q % 4, q // 4]
+                    out=raw[:, m * 2048 : (m + 1) * 2048],
+                    in_=wviews[m][LAST_LOADS[q - 12] if q >= 12 else q % 4, q // 4],
                 )
-            raws[q] = raw
+            raws[q // 4, LAST_LOADS[q - 12] if q >= 12 else q % 4] = raw
+
+        def parts(q):
+            return LAST_PARTS[q - 12] if q >= 12 else [(q % 4, 0), (q % 4, 1)]
 
         def copy_out(on_vector, out_ap, in_ap):
             if on_vector:
@@ -166,7 +172,7 @@ def tile_network_pb_kernel(
 
         def acts_unit():
             words = raws["acts"][:].bitcast(F32)
-            grp = grpp.tile([P, 4096], BF16, tag="grp", name="grp", align_bytes=64)
+            grp = grpp.tile([P, 4096], BF16, tag="grp", name="grp", align_bytes=256)
             grpf = grp[:].bitcast(F32)
             for c in range(4):
                 m, bt = c // 2, c % 2
@@ -180,15 +186,15 @@ def tile_network_pb_kernel(
             grps["acts"] = grp
 
         def unit_transposes(q):
-            words = raws[q][:].bitcast(F32)
-            grp = grpp.tile([P, 4096], BF16, tag="grp", name="grp", align_bytes=64)
+            grp = grpp.tile([P, 4096], BF16, tag="grp", name="grp", align_bytes=256)
             grpf = grp[:].bitcast(F32)
-            cod = codp.tile([P, 1024], U32, tag="cod", name="cod", align_bytes=64)
-            scl = codp.tile([P, 1024], U8, tag="scl", name="scl", align_bytes=64)
+            cod = codp.tile([P, 1024], U32, tag="cod", name="cod", align_bytes=256)
+            scl = codp.tile([P, 1024], U8, tag="scl", name="scl", align_bytes=256)
             grps[q] = grp
             codes[q] = (cod, scl)
             for c in range(4):
-                e, m = c // 2, c % 2
+                (gate, e), m = parts(q)[c // 2], c % 2
+                words = raws[q // 4, gate][:].bitcast(F32)
                 tp = t_bank(four(words, m * 1024 + e * 512))
                 copy_out(c == 2, pair_dst(grpf[:, c * 512 : (c + 1) * 512]), pairs(tp))
                 if c == 2:
@@ -231,7 +237,7 @@ def tile_network_pb_kernel(
                 )
                 return
             tp = t_bank(four(words, 0))
-            sgrp = sgrpp.tile([P, 1024], BF16, tag="sgrp", name="sgrp", align_bytes=64)
+            sgrp = sgrpp.tile([P, 1024], BF16, tag="sgrp", name="sgrp", align_bytes=256)
             copy_out(on_vector, pair_dst(sgrp[:].bitcast(F32)), pairs(tp))
             sgrps[q] = sgrp
 
@@ -287,8 +293,8 @@ def tile_network_pb_kernel(
                 mx(dp[:, e, :], dcod, dscl, (2 * jj + e) * P, xcod, xscl, 0, B, True, True)
             dps[jj] = dp
 
-        def gate_function(q, e, in_ap):
-            jj, gate = q // 4, q % 4
+        def gate_function(q, part, in_ap):
+            jj, (gate, e) = q // 4, parts(q)[part]
             col = (gate * 4 + jj) * 2 + e
             nc.scalar.activation(
                 out=gacts[jj][:, gate, e, :],
@@ -350,6 +356,11 @@ def tile_network_pb_kernel(
                 if jj > 0:
                     skip_sum(jj - 1, 0)
                     skip_sum(jj - 1, 1)
+                if jj == 3:
+                    last_ig(0)
+                return
+            if jj == 3:
+                last_fc(0)
                 return
             ga, t = gacts[jj], cell[jj]
             if gate == 1:
@@ -369,9 +380,34 @@ def tile_network_pb_kernel(
             jj, gate = q // 4, q % 4
             if gate == 0 and jj > 0:
                 mid_regroup(jj - 1)
+            elif jj == 3:
+                last_cn(0)
             elif gate == 2:
                 t = cell[jj]
                 cell_tt(jj, t["cn"][:], t["fc"][:], t["ig"][:], ALU.add)
+
+        def last_ig(e):
+            nc.vector.tensor_tensor(
+                out=cell[3]["ig"][:, e, :], in0=gacts[3][:, 0, e, :], in1=gacts[3][:, 2, e, :],
+                op=ALU.mult,
+            )
+
+        def last_fc(e):
+            cv = cT[:].bitcast(BF16)[:, 3, :].rearrange("p (b e) -> p e b", e=2)
+            nc.vector.tensor_tensor(
+                out=cell[3]["fc"][:, e, :], in0=gacts[3][:, 1, e, :], in1=cv[:, e, :], op=ALU.mult
+            )
+
+        def last_cn(e):
+            nc.vector.tensor_tensor(
+                out=cell[3]["cn"][:, e, :], in0=cell[3]["fc"][:, e, :], in1=cell[3]["ig"][:, e, :],
+                op=ALU.add,
+            )
+
+        def last_th(e):
+            nc.scalar.activation(
+                out=cell[3]["th"][:, e, :], in_=cell[3]["cn"][:, e, :], func=AF.Tanh
+            )
 
         def out_transposes(jj, bt):
             ot = tpp.tile([P, 4, P], F32, tag="tp", name="ot")
@@ -420,12 +456,15 @@ def tile_network_pb_kernel(
 
         wm_banks = [wm_bank(b) for b in range(2)]
         quant_rest(UNITS - 1)
-        for q in range(UNITS - LAG - 1, UNITS - 1):
-            gate_functions(q)
-            cell_work(q)
-            cell_work_late(q)
-            gate_passes(q + 1)
-        wm_copy(0, wm_banks[0])
+        gate_functions(UNITS - 2)
+        last_th(0)
+        last_ig(1)
+        last_fc(1)
+        last_cn(1)
+        for b in range(2):
+            wm_copy(b, wm_banks[b])
+        wm_quant(0)
+        last_th(1)
         o_banks = []
         for e in range(2):
             ob = tpp.tile([P, B], F32, tag="tp", name="ob")
@@ -435,17 +474,8 @@ def tile_network_pb_kernel(
         wm_banks += [wm_bank(b) for b in range(2, 4)]
         ga, t = gacts[3], cell[3]
         for e in range(2):
-            nc.vector.tensor_tensor(
-                out=t["ig"][:, e, :], in0=ga[:, 0, e, :], in1=ga[:, 2, e, :], op=ALU.mult
-            )
-        for e in range(2):
-            nc.vector.tensor_tensor(
-                out=t["cn"][:, e, :], in0=t["fc"][:, e, :], in1=t["ig"][:, e, :], op=ALU.add
-            )
-        for e in range(2):
             gate_function(15, e, o_banks[e][:])
-            nc.scalar.activation(out=t["th"][:, e, :], in_=t["cn"][:, e, :], func=AF.Tanh)
-        for b in range(1, 4):
+        for b in range(2, 4):
             wm_copy(b, wm_banks[b])
         outs = [(jj, bt) for jj in range(4) for bt in range(2)]
         banks = [out_transposes(jj, bt) for jj, bt in outs[0:3]]
@@ -455,9 +485,8 @@ def tile_network_pb_kernel(
             )
         for e in range(2):
             skip_sum(3, e)
-        wm_quant(0)
-        mid_regroup(3)
         wm_quant(1)
+        mid_regroup(3)
         quant_mid(1)
         mps = []
         for bt in range(2):

@@ -42,7 +42,7 @@ def tile_network_pb_kernel(
         gactp = ctx.enter_context(tc.tile_pool(name="gactp", bufs=2))
         ew1 = ctx.enter_context(tc.tile_pool(name="ew1", bufs=1))
         ew4 = ctx.enter_context(tc.tile_pool(name="ew4", bufs=4))
-        resp = ctx.enter_context(tc.tile_pool(name="resp", bufs=8))
+        resp = ctx.enter_context(tc.tile_pool(name="resp", bufs=4))
         tpp = ctx.enter_context(tc.psum_pool(name="tpp", bufs=5))
         gtp = ctx.enter_context(tc.psum_pool(name="gtp", bufs=3))
         ctx.enter_context(tc.manual_schedule())
@@ -169,6 +169,7 @@ def tile_network_pb_kernel(
         cell = {}
         dps = {}
         sgrps = {}
+        ress = {}
 
         def acts_unit():
             words = raws["acts"][:].bitcast(F32)
@@ -420,16 +421,20 @@ def tile_network_pb_kernel(
 
         def out_store(item, on_vector):
             jj, bt, ot = item
-            res = resp.tile([P, 2, B], F32, tag="res", name="res")
+            if jj % 2 == 0:
+                ress[bt] = resp.tile([P, 2, 2 * B], F32, tag="res", name="res")
+            res = ress[bt]
+            half = slice(jj % 2 * B, (jj % 2 + 1) * B)
             copy_out(
                 on_vector,
-                res[:].rearrange("b s (p e) -> b s p e", e=2),
+                res[:, :, half].rearrange("b s (p e) -> b s p e", e=2),
                 ot[:].rearrange("b (s e) p -> b s p e", s=2, e=2),
             )
-            rows = slice(bt * P, (bt + 1) * P)
-            cols = slice(jj * B, (jj + 1) * B)
-            nc.sync.dma_start(out=out_1[rows, cols], in_=res[:, 0, :])
-            nc.sync.dma_start(out=out_2[rows, cols], in_=res[:, 1, :])
+            if jj % 2 == 1:
+                rows = slice(bt * P, (bt + 1) * P)
+                cols = slice((jj - 1) * B, (jj + 1) * B)
+                nc.sync.dma_start(out=out_1[rows, cols], in_=res[:, 0, :])
+                nc.sync.dma_start(out=out_2[rows, cols], in_=res[:, 1, :])
 
         load_acts()
         for q in range(RAW_BUFS - 1):
@@ -477,7 +482,7 @@ def tile_network_pb_kernel(
             gate_function(15, e, o_banks[e][:])
         for b in range(2, 4):
             wm_copy(b, wm_banks[b])
-        outs = [(jj, bt) for jj in range(4) for bt in range(2)]
+        outs = [(2 * g + u, bt) for g in range(2) for bt in range(2) for u in range(2)]
         banks = [out_transposes(jj, bt) for jj, bt in outs[0:3]]
         for e in range(2):
             nc.vector.tensor_tensor(

@@ -76,11 +76,11 @@ def tile_network_pb_kernel(
         wmscl = const.tile([P, 1024], U8, align_bytes=256)
         mcod = const.tile([P, 512], U32, align_bytes=256)
         mscl = const.tile([P, 512], U8, align_bytes=256)
-        cT = const.tile([P, 4, 256], F32)
+        cT = const.tile([P, 4, 256], F32, align_bytes=256)
         bT = const.tile([P, 72], F32)
         bsum = const.tile([P, 32], F32)
-        bmbc = const.tile([P, 512], F32)
-        midT = const.tile([P, 2, 4, 256], BF16)
+        bmbc = const.tile([P, 512], F32, align_bytes=256)
+        midT = const.tile([P, 2, 4, 256], BF16, align_bytes=256)
         midgrp = const.tile([P, 2, 1024], BF16, align_bytes=256)
 
         wviews = [
@@ -309,7 +309,7 @@ def tile_network_pb_kernel(
             if not 0 <= q < UNITS - 1:
                 return
             if q % 4 == 0:
-                gacts[q // 4] = gactp.tile([P, 4, 2, B], F32, tag="gact", name="gact")
+                gacts[q // 4] = gactp.tile([P, 4, 2, B], F32, tag="gact", name="gact", align_bytes=256)
             for e in range(2):
                 gate_function(q, e, gts[q][:, e, :])
 
@@ -321,11 +321,11 @@ def tile_network_pb_kernel(
 
         def new_cell_tiles(jj):
             cell[jj] = {
-                "fc": ew1.tile([P, 2, B], F32, tag="fc", name="fc"),
-                "ig": ew1.tile([P, 2, B], F32, tag="ig", name="ig"),
-                "th": ew1.tile([P, 2, B], F32, tag="th", name="th"),
-                "cn": ew4.tile([P, 2, B], F32, tag="cn", name="cn"),
-                "y": ew4.tile([P, 2, B], F32, tag="y", name="y"),
+                "fc": ew1.tile([P, 2, B], F32, tag="fc", name="fc", align_bytes=256),
+                "ig": ew1.tile([P, 2, B], F32, tag="ig", name="ig", align_bytes=256),
+                "th": ew1.tile([P, 2, B], F32, tag="th", name="th", align_bytes=256),
+                "cn": ew4.tile([P, 2, B], F32, tag="cn", name="cn", align_bytes=256),
+                "y": ew4.tile([P, 2, B], F32, tag="y", name="y", align_bytes=256),
             }
 
         def skip_sum(jj, e):
@@ -422,7 +422,7 @@ def tile_network_pb_kernel(
         def out_store(item, on_vector):
             jj, bt, ot = item
             if jj % 2 == 0:
-                ress[bt] = resp.tile([P, 2, 2 * B], F32, tag="res", name="res")
+                ress[bt] = resp.tile([P, 2, 2 * B], F32, tag="res", name="res", align_bytes=256)
             res = ress[bt]
             half = slice(jj % 2 * B, (jj % 2 + 1) * B)
             copy_out(
@@ -469,7 +469,6 @@ def tile_network_pb_kernel(
         for b in range(2):
             wm_copy(b, wm_banks[b])
         wm_quant(0)
-        last_th(1)
         o_banks = []
         for e in range(2):
             ob = tpp.tile([P, B], F32, tag="tp", name="ob")
@@ -478,8 +477,9 @@ def tile_network_pb_kernel(
         skip_passes(3)
         wm_banks += [wm_bank(b) for b in range(2, 4)]
         ga, t = gacts[3], cell[3]
-        for e in range(2):
-            gate_function(15, e, o_banks[e][:])
+        gate_function(15, 0, o_banks[0][:])
+        last_th(1)
+        gate_function(15, 1, o_banks[1][:])
         for b in range(2, 4):
             wm_copy(b, wm_banks[b])
         outs = [(2 * g + u, bt) for g in range(2) for bt in range(2) for u in range(2)]
@@ -490,26 +490,25 @@ def tile_network_pb_kernel(
             )
         for e in range(2):
             skip_sum(3, e)
-        wm_quant(1)
         mid_regroup(3)
+        wm_quant(1)
         quant_mid(1)
+        more = [out_transposes(jj, bt) for jj, bt in outs[3:5]]
         mps = []
         for bt in range(2):
             mp = gtp.tile([P, 512], F32, tag="gt", name="mp")
             mx(mp[:], mcod, mscl, bt * P, wmcod, wmscl, 0, 512, True, False)
             mps.append(mp)
-        for item in banks:
+        for item in banks + more[:1]:
             out_store(item, False)
-        banks = [out_transposes(jj, bt) for jj, bt in outs[3:5]]
-        out_store(banks[0], False)
         nc.scalar.activation(out=tiny_out[:], in_=tiny_in[:], func=AF.Exp)
         for bt in range(2):
             mx(mps[bt][:], mcod, mscl, B + bt * P, wmcod, wmscl, 512, 512, False, True)
-        out_store(banks[1], True)
+        out_store(more[1], True)
         banks = [out_transposes(jj, bt) for jj, bt in outs[5:8]]
         ssum = const.tile([P, 2], F32)
         lsum = const.tile([P, 2], F32)
-        ex = const.tile([P, 512], F32)
+        ex = const.tile([P, 512], F32, align_bytes=256)
         mots = []
         nmxs = []
         for bt in range(2):

@@ -56,10 +56,6 @@ def tile_network_pb_kernel(
         nc.vector.memset(braw[:], 0.0)
         nc.vector.memset(bmrow[:], 0.0)
         nc.vector.memset(tiny_in[:], 0.0)
-        nc.scalar.dma_start(out=braw[0:16, :], in_=bih3.rearrange("(r c) -> r c", c=256))
-        nc.scalar.dma_start(out=braw[16:32, :], in_=bhh3.rearrange("(r c) -> r c", c=256))
-        nc.scalar.dma_start(out=braw[32:36, :], in_=bd.rearrange("(r c) -> r c", c=256))
-        nc.scalar.dma_start(out=bmrow[0:1, :], in_=bm.rearrange("(o m) -> o m", o=1))
         nc.scalar.activation(out=tiny_out[:], in_=tiny_in[:], func=AF.Sigmoid)
         ident = const.tile([P, P], F32, align_bytes=256)
         make_identity(nc, ident[:])
@@ -102,6 +98,13 @@ def tile_network_pb_kernel(
         def load_unit(q):
             if q >= UNITS:
                 return
+            raw = rawp.tile([P, 4096], BF16, tag="raw", name="raw", align_bytes=256)
+            for m in range(2):
+                nc.sync.dma_start(
+                    out=raw[:, m * 2048 : (m + 1) * 2048],
+                    in_=wviews[m][LAST_LOADS[q - 12] if q >= 12 else q % 4, q // 4],
+                )
+            raws[q // 4, LAST_LOADS[q - 12] if q >= 12 else q % 4] = raw
             job = SMALL[q]
             if job is not None and job[0] != "bias":
                 kind, i = job
@@ -116,13 +119,6 @@ def tile_network_pb_kernel(
                     src = Wd.rearrange("(j p e) k -> j p (e k)", j=4, p=P, e=2)
                     nc.sync.dma_start(out=sraw[:], in_=src[i])
                 sraws[q] = sraw
-            raw = rawp.tile([P, 4096], BF16, tag="raw", name="raw", align_bytes=256)
-            for m in range(2):
-                nc.sync.dma_start(
-                    out=raw[:, m * 2048 : (m + 1) * 2048],
-                    in_=wviews[m][LAST_LOADS[q - 12] if q >= 12 else q % 4, q // 4],
-                )
-            raws[q // 4, LAST_LOADS[q - 12] if q >= 12 else q % 4] = raw
 
         def parts(q):
             return LAST_PARTS[q - 12] if q >= 12 else [(q % 4, 0), (q % 4, 1)]
@@ -197,7 +193,7 @@ def tile_network_pb_kernel(
                 (gate, e), m = parts(q)[c // 2], c % 2
                 words = raws[q // 4, gate][:].bitcast(F32)
                 tp = t_bank(four(words, m * 1024 + e * 512))
-                copy_out(c == 2, pair_dst(grpf[:, c * 512 : (c + 1) * 512]), pairs(tp))
+                copy_out(c == 2 and (q == 0 or q % 4 != 0), pair_dst(grpf[:, c * 512 : (c + 1) * 512]), pairs(tp))
                 if c == 2:
                     quant(cod[:, 0:512], scl[:, 0:512], grp[:, 0:2048])
 
@@ -437,7 +433,12 @@ def tile_network_pb_kernel(
                 nc.sync.dma_start(out=out_2[rows, cols], in_=res[:, 1, :])
 
         load_acts()
-        for q in range(RAW_BUFS - 1):
+        load_unit(0)
+        nc.sync.dma_start(out=braw[0:16, :], in_=bih3.rearrange("(r c) -> r c", c=256))
+        nc.sync.dma_start(out=braw[16:32, :], in_=bhh3.rearrange("(r c) -> r c", c=256))
+        nc.sync.dma_start(out=braw[32:36, :], in_=bd.rearrange("(r c) -> r c", c=256))
+        nc.sync.dma_start(out=bmrow[0:1, :], in_=bm.rearrange("(o m) -> o m", o=1))
+        for q in range(1, RAW_BUFS - 1):
             load_unit(q)
         acts_unit()
         load_unit(RAW_BUFS - 1)

from contextlib import ExitStack

import concourse.mybir as mybir
from concourse.masks import make_identity

F32 = mybir.dt.float32
BF16 = mybir.dt.bfloat16
U32 = mybir.dt.uint32
U8 = mybir.dt.uint8
FP8X4 = mybir.dt.float8_e4m3fn_x4
AF = mybir.ActivationFunctionType
ALU = mybir.AluOpType
AX = mybir.AxisListType

P = 128
B = 256
UNITS = 16
FLOPS = 2 * 256 * (4096 * 2048 + 1024 * 512 + 512 * 1024)

RAW_BUFS = 8
LAG = 1
CELL_ON_GPSIMD = False
LAST_PARTS = [[(0, 0), (2, 0)], [(1, 0), (0, 1)], [(2, 1), (1, 1)], [(3, 0), (3, 1)]]
LAST_LOADS = [0, 2, 1, 3]
SMALL = [
    ("bias", 0), None, ("c3", 0), ("x", 0), ("Wd", 0), None, None, ("Wd", 1),
    None, ("c3", 1), None, ("Wd", 2), None, ("Wd", 3), None, None,
]


def tile_network_pb_kernel(
    tc, x, y2, h3, c3, Wih3, Whh3, bih3, bhh3, Wd, bd, Wm, bm, out_0, out_1, out_2
):
    nc = tc.nc
    with ExitStack() as ctx:
        const = ctx.enter_context(tc.tile_pool(name="const", bufs=1))
        rawp = ctx.enter_context(tc.tile_pool(name="rawp", bufs=RAW_BUFS))
        srawp = ctx.enter_context(tc.tile_pool(name="srawp", bufs=4))
        grpp = ctx.enter_context(tc.tile_pool(name="grpp", bufs=3))
        sgrpp = ctx.enter_context(tc.tile_pool(name="sgrpp", bufs=2))
        codp = ctx.enter_context(tc.tile_pool(name="codp", bufs=4))
        gactp = ctx.enter_context(tc.tile_pool(name="gactp", bufs=2))
        ew1 = ctx.enter_context(tc.tile_pool(name="ew1", bufs=1))
        ew4 = ctx.enter_context(tc.tile_pool(name="ew4", bufs=4))
        resp = ctx.enter_context(tc.tile_pool(name="resp", bufs=4))
        tpp = ctx.enter_context(tc.psum_pool(name="tpp", bufs=5))
        gtp = ctx.enter_context(tc.psum_pool(name="gtp", bufs=3))
        ctx.enter_context(tc.manual_schedule())

        ones = const.tile([P, P], BF16)
        braw = const.tile([P, 256], BF16)
        bmrow = const.tile([P, 512], BF16)
        tiny_in = const.tile([P, 1], F32)
        tiny_out = const.tile([P, 1], F32)
        nc.vector.memset(ones[:], 1.0)
        nc.vector.memset(braw[:], 0.0)
        nc.vector.memset(bmrow[:], 0.0)
        nc.vector.memset(tiny_in[:], 0.0)
        nc.scalar.activation(out=tiny_out[:], in_=tiny_in[:], func=AF.Sigmoid)
        ident = const.tile([P, P], F32, align_bytes=256)
        make_identity(nc, ident[:])

        acod = const.tile([P, 1024], U32, align_bytes=256)
        ascl = const.tile([P, 1024], U8, align_bytes=256)
        xcod = const.tile([P, 256], U32, align_bytes=256)
        xscl = const.tile([P, 256], U8, align_bytes=256)
        dcod = const.tile([P, 1024], U32, align_bytes=256)
        dscl = const.tile([P, 1024], U8, align_bytes=256)
        wmraw = const.tile([P, 4096], BF16, align_bytes=256)
        wmgrp = const.tile([P, 4096], BF16, align_bytes=256)
        wmcod = const.tile([P, 1024], U32, align_bytes=256)
        wmscl = const.tile([P, 1024], U8, align_bytes=256)
        mcod = const.tile([P, 512], U32, align_bytes=256)
        mscl = const.tile([P, 512], U8, align_bytes=256)
        cT = const.tile([P, 4, 256], F32, align_bytes=256)
        bT = const.tile([P, 72], F32)
        bsum = const.tile([P, 32], F32)
        bmbc = const.tile([P, 512], F32, align_bytes=256)
        midT = const.tile([P, 2, 4, 256], BF16, align_bytes=256)
        midgrp = const.tile([P, 2, 1024], BF16, align_bytes=256)

        wviews = [
            w.rearrange("(g j p e) k -> g j p (e k)", g=4, j=4, p=P, e=2) for w in (Wih3, Whh3)
        ]
        raws = {}
        sraws = {}

        def load_acts():
            raw = rawp.tile([P, 4096], BF16, tag="raw", name="raw", align_bytes=256)
            for m, src in enumerate((y2, h3)):
                for t in range(2):
                    c0 = (2 * m + t) * 1024
                    nc.sync.dma_start(
                        out=raw[:, c0 : c0 + 1024], in_=src[t * P : (t + 1) * P, :]
                    )
            raws["acts"] = raw

        def load_unit(q):
            if q >= UNITS:
                return
            raw = rawp.tile([P, 4096], BF16, tag="raw", name="raw", align_bytes=256)
            for m in range(2):
                nc.sync.dma_start(
                    out=raw[:, m * 2048 : (m + 1) * 2048],
                    in_=wviews[m][LAST_LOADS[q - 12] if q >= 12 else q % 4, q // 4],
                )
            raws[q // 4, LAST_LOADS[q - 12] if q >= 12 else q % 4] = raw
            job = SMALL[q]
            if job is not None and job[0] != "bias":
                kind, i = job
                sraw = srawp.tile([P, 1024], BF16, tag="sraw", name="sraw", align_bytes=256)
                two = sraw[:].rearrange("p (t k) -> p t k", t=2)
                if kind == "c3":
                    src = c3.rearrange("(t p) k -> p t k", p=P)[:, :, i * 512 : (i + 1) * 512]
                    nc.sync.dma_start(out=two, in_=src)
                elif kind == "x":
                    nc.sync.dma_start(out=two, in_=x.rearrange("(t p) k -> p t k", p=P))
                else:
                    src = Wd.rearrange("(j p e) k -> j p (e k)", j=4, p=P, e=2)
                    nc.sync.dma_start(out=sraw[:], in_=src[i])
                sraws[q] = sraw

        def parts(q):
            return LAST_PARTS[q - 12] if q >= 12 else [(q % 4, 0), (q % 4, 1)]

        def copy_out(on_vector, out_ap, in_ap):
            if on_vector:
                nc.vector.tensor_copy(out=out_ap, in_=in_ap)
            else:
                nc.scalar.copy(out=out_ap, in_=in_ap)

        def t_bank(srcs):
            tp = tpp.tile([P, 4, P], F32, tag="tp", name="tp")
            for n, s in enumerate(srcs):
                nc.tensor.transpose(tp[:, n, :], s, ident[:])
            return tp

        def four(words, w0):
            return [words[:, w0 + n * P : w0 + (n + 1) * P] for n in range(4)]

        def pairs(tp):
            return tp[:].rearrange("w (a u) p -> w a p u", a=2, u=2)

        def pair_dst(ap):
            return ap.rearrange("w (a p u) -> w a p u", a=2, p=P, u=2)

        def quant(cod_ap, scl_ap, in_ap):
            nc.vector.quantize_mx(out=cod_ap.bitcast(FP8X4), scales=scl_ap, in_=in_ap)

        def mx(out_ap, l_cod, l_scl, l0, r_cod, r_scl, r0, n, start, stop):
            nc.tensor.matmul_mx(
                out=out_ap,
                lhsT=l_cod[:, l0 : l0 + P].bitcast(FP8X4),
                lhsT_scale=l_scl[:, l0 : l0 + P],
                rhs=r_cod[:, r0 : r0 + n].bitcast(FP8X4),
                rhs_scale=r_scl[:, r0 : r0 + n],
                start=start,
                stop=stop,
            )

        grps = {}
        codes = {}
        gts = {}
        gacts = {}
        cell = {}
        dps = {}
        sgrps = {}
        ress = {}

        def acts_unit():
            words = raws["acts"][:].bitcast(F32)
            grp = grpp.tile([P, 4096], BF16, tag="grp", name="grp", align_bytes=256)
            grpf = grp[:].bitcast(F32)
            for c in range(4):
                m, bt = c // 2, c % 2
                tp = t_bank(four(words, c * 512))
                dst = grpf[:, m * 1024 : (m + 1) * 1024].rearrange(
                    "w (a b u) -> w a b u", a=2, b=B, u=2
                )
                copy_out(c % 2 == 0, dst[:, :, bt * P : (bt + 1) * P, :], pairs(tp))
                if c == 2:
                    quant(acod[:, 0:512], ascl[:, 0:512], grp[:, 0:2048])
            grps["acts"] = grp

        def unit_transposes(q):
            grp = grpp.tile([P, 4096], BF16, tag="grp", name="grp", align_bytes=256)
            grpf = grp[:].bitcast(F32)
            cod = codp.tile([P, 1024], U32, tag="cod", name="cod", align_bytes=256)
            scl = codp.tile([P, 1024], U8, tag="scl", name="scl", align_bytes=256)
            grps[q] = grp
            codes[q] = (cod, scl)
            for c in range(4):
                (gate, e), m = parts(q)[c // 2], c % 2
                words = raws[q // 4, gate][:].bitcast(F32)
                tp = t_bank(four(words, m * 1024 + e * 512))
                copy_out(c == 2 and (q == 0 or q % 4 != 0), pair_dst(grpf[:, c * 512 : (c + 1) * 512]), pairs(tp))
                if c == 2:
                    quant(cod[:, 0:512], scl[:, 0:512], grp[:, 0:2048])

        def quant_rest(q):
            if q == -1:
                quant(acod[:, 512:1024], ascl[:, 512:1024], grps["acts"][:, 2048:4096])
            elif 0 <= q < UNITS:
                cod, scl = codes[q]
                quant(cod[:, 512:1024], scl[:, 512:1024], grps[q][:, 2048:4096])

        def small_bank(q):
            job = SMALL[q]
            if job is None:
                return
            kind, i = job
            on_vector = False
            if kind == "bias":
                tp = t_bank([braw[:].bitcast(F32)])
                nc.vector.tensor_copy(out=bT[:], in_=tp[:].bitcast(BF16)[:, 0, 0:72])
                nc.vector.tensor_tensor(out=bsum[:], in0=bT[:, 0:32], in1=bT[:, 32:64], op=ALU.add)
                bmp = tpp.tile([P, 512], F32, tag="tp", name="bmp")
                nc.tensor.matmul(out=bmp[:], lhsT=ones[:], rhs=bmrow[:], start=True, stop=True)
                copy_out(False, bmbc[:], bmp[:])
                return
            words = sraws[q][:].bitcast(F32)
            if kind == "c3":
                tp = t_bank(
                    [
                        words[:, bt * 256 + jl * P : bt * 256 + (jl + 1) * P]
                        for jl in range(2)
                        for bt in range(2)
                    ]
                )
                copy_out(
                    on_vector,
                    cT[:, 2 * i : 2 * i + 2, :].rearrange("w a b -> w (a b)"),
                    tp[:].rearrange("w n p -> w (n p)"),
                )
                return
            tp = t_bank(four(words, 0))
            sgrp = sgrpp.tile([P, 1024], BF16, tag="sgrp", name="sgrp", align_bytes=256)
            copy_out(on_vector, pair_dst(sgrp[:].bitcast(F32)), pairs(tp))
            sgrps[q] = sgrp

        def small_quant(q):
            job = SMALL[q] if q >= 0 else None
            if job is None:
                return
            kind, i = job
            if kind == "x":
                quant(xcod[:], xscl[:], sgrps[q][:])
            elif kind == "Wd":
                quant(dcod[:, i * 256 : (i + 1) * 256], dscl[:, i * 256 : (i + 1) * 256], sgrps[q][:])

        def wm_bank(b):
            a, h = b // 2, b % 2
            words = wmraw[:].bitcast(F32)
            return t_bank(
                [
                    words[:, i * 512 + (2 * a + u) * P : i * 512 + (2 * a + u + 1) * P]
                    for i in (2 * h, 2 * h + 1)
                    for u in range(2)
                ]
            )

        def wm_copy(b, tp):
            copy_out(False, pair_dst(wmgrp[:].bitcast(F32)[:, b * 512 : (b + 1) * 512]), pairs(tp))

        def wm_quant(a):
            half = slice(a * 512, (a + 1) * 512)
            quant(wmcod[:, half], wmscl[:, half], wmgrp[:, a * 2048 : (a + 1) * 2048])

        def gate_group(out_ap, q, e):
            cod, scl = codes[q]
            for m in range(2):
                for g in range(2):
                    mx(
                        out_ap, cod, scl, ((e * 2 + m) * 2 + g) * P,
                        acod, ascl, m * 512 + g * B, B,
                        (m == 0 and g == 0), (m == 1 and g == 1),
                    )

        def gate_passes(q):
            if not 0 <= q < UNITS - 1:
                return
            gt = gtp.tile([P, 2, B], F32, tag="gt", name="gt")
            for e in range(2):
                gate_group(gt[:, e, :], q, e)
            gts[q] = gt

        def skip_passes(jj):
            dp = gtp.tile([P, 2, B], F32, tag="gt", name="dp")
            for e in range(2):
                mx(dp[:, e, :], dcod, dscl, (2 * jj + e) * P, xcod, xscl, 0, B, True, True)
            dps[jj] = dp

        def gate_function(q, part, in_ap):
            jj, (gate, e) = q // 4, parts(q)[part]
            col = (gate * 4 + jj) * 2 + e
            nc.scalar.activation(
                out=gacts[jj][:, gate, e, :],
                in_=in_ap,
                func=(AF.Tanh if gate == 2 else AF.Sigmoid),
                bias=bsum[:, col : col + 1],
                scale=1.0,
            )

        def gate_functions(q):
            if not 0 <= q < UNITS - 1:
                return
            if q % 4 == 0:
                gacts[q // 4] = gactp.tile([P, 4, 2, B], F32, tag="gact", name="gact", align_bytes=256)
            for e in range(2):
                gate_function(q, e, gts[q][:, e, :])

        def cell_tt(jj, out_ap, in0, in1, op):
            if CELL_ON_GPSIMD and jj < 3:
                nc.gpsimd.tensor_tensor(out=out_ap, in0=in0, in1=in1, op=op)
            else:
                nc.vector.tensor_tensor(out=out_ap, in0=in0, in1=in1, op=op)

        def new_cell_tiles(jj):
            cell[jj] = {
                "fc": ew1.tile([P, 2, B], F32, tag="fc", name="fc", align_bytes=256),
                "ig": ew1.tile([P, 2, B], F32, tag="ig", name="ig", align_bytes=256),
                "th": ew1.tile([P, 2, B], F32, tag="th", name="th", align_bytes=256),
                "cn": ew4.tile([P, 2, B], F32, tag="cn", name="cn", align_bytes=256),
                "y": ew4.tile([P, 2, B], F32, tag="y", name="y", align_bytes=256),
            }

        def skip_sum(jj, e):
            nc.vector.scalar_tensor_tensor(
                out=midT[:, jj // 2, 2 * (jj % 2) + e, :],
                in0=dps[jj][:, e, :],
                scalar=bT[:, 64 + 2 * jj + e : 65 + 2 * jj + e],
                in1=cell[jj]["y"][:, e, :],
                op0=ALU.add,
                op1=ALU.add,
            )

        def mid_regroup(jj):
            g, uu = jj // 2, jj % 2
            nc.vector.tensor_copy(
                out=midgrp[:, g, :].rearrange("p (b t) -> p b t", t=4)[:, :, 2 * uu : 2 * uu + 2],
                in_=midT[:, g, 2 * uu : 2 * uu + 2, :].rearrange("p t b -> p b t"),
            )

        def quant_mid(g):
            quant(mcod[:, g * B : (g + 1) * B], mscl[:, g * B : (g + 1) * B], midgrp[:, g, :])

        def cell_work(q):
            if not 0 <= q < UNITS - 2:
                return
            jj, gate = q // 4, q % 4
            if gate == 0:
                new_cell_tiles(jj)
                if jj > 0:
                    skip_sum(jj - 1, 0)
                    skip_sum(jj - 1, 1)
                if jj == 3:
                    last_ig(0)
                return
            if jj == 3:
                last_fc(0)
                return
            ga, t = gacts[jj], cell[jj]
            if gate == 1:
                if jj == 2:
                    quant_mid(0)
                cv = cT[:].bitcast(BF16)[:, jj, :].rearrange("p (b e) -> p e b", e=2)
                cell_tt(jj, t["fc"][:], ga[:, 1, :, :], cv, ALU.mult)
            elif gate == 2:
                cell_tt(jj, t["ig"][:], ga[:, 0, :, :], ga[:, 2, :, :], ALU.mult)
            else:
                nc.scalar.activation(out=t["th"][:], in_=t["cn"][:], func=AF.Tanh)
                cell_tt(jj, t["y"][:], ga[:, 3, :, :], t["th"][:], ALU.mult)

        def cell_work_late(q):
            if not 0 <= q < UNITS - 2:
                return
            jj, gate = q // 4, q % 4
            if gate == 0 and jj > 0:
                mid_regroup(jj - 1)
            elif jj == 3:
                last_cn(0)
            elif gate == 2:
                t = cell[jj]
                cell_tt(jj, t["cn"][:], t["fc"][:], t["ig"][:], ALU.add)

        def last_ig(e):
            nc.vector.tensor_tensor(
                out=cell[3]["ig"][:, e, :], in0=gacts[3][:, 0, e, :], in1=gacts[3][:, 2, e, :],
                op=ALU.mult,
            )

        def last_fc(e):
            cv = cT[:].bitcast(BF16)[:, 3, :].rearrange("p (b e) -> p e b", e=2)
            nc.vector.tensor_tensor(
                out=cell[3]["fc"][:, e, :], in0=gacts[3][:, 1, e, :], in1=cv[:, e, :], op=ALU.mult
            )

        def last_cn(e):
            nc.vector.tensor_tensor(
                out=cell[3]["cn"][:, e, :], in0=cell[3]["fc"][:, e, :], in1=cell[3]["ig"][:, e, :],
                op=ALU.add,
            )

        def last_th(e):
            nc.scalar.activation(
                out=cell[3]["th"][:, e, :], in_=cell[3]["cn"][:, e, :], func=AF.Tanh
            )

        def out_transposes(jj, bt):
            ot = tpp.tile([P, 4, P], F32, tag="tp", name="ot")
            for si, key in enumerate(("y", "cn")):
                for e in range(2):
                    nc.tensor.transpose(
                        ot[:, si * 2 + e, :], cell[jj][key][:, e, bt * P : (bt + 1) * P], ident[:]
                    )
            return (jj, bt, ot)

        def out_store(item, on_vector):
            jj, bt, ot = item
            if jj % 2 == 0:
                ress[bt] = resp.tile([P, 2, 2 * B], F32, tag="res", name="res", align_bytes=256)
            res = ress[bt]
            half = slice(jj % 2 * B, (jj % 2 + 1) * B)
            copy_out(
                on_vector,
                res[:, :, half].rearrange("b s (p e) -> b s p e", e=2),
                ot[:].rearrange("b (s e) p -> b s p e", s=2, e=2),
            )
            if jj % 2 == 1:
                rows = slice(bt * P, (bt + 1) * P)
                cols = slice((jj - 1) * B, (jj + 1) * B)
                nc.sync.dma_start(out=out_1[rows, cols], in_=res[:, 0, :])
                nc.sync.dma_start(out=out_2[rows, cols], in_=res[:, 1, :])

        load_acts()
        load_unit(0)
        nc.sync.dma_start(out=braw[0:16, :], in_=bih3.rearrange("(r c) -> r c", c=256))
        nc.sync.dma_start(out=braw[16:32, :], in_=bhh3.rearrange("(r c) -> r c", c=256))
        nc.sync.dma_start(out=braw[32:36, :], in_=bd.rearrange("(r c) -> r c", c=256))
        nc.sync.dma_start(out=bmrow[0:1, :], in_=bm.rearrange("(o m) -> o m", o=1))
        for q in range(1, RAW_BUFS - 1):
            load_unit(q)
        acts_unit()
        load_unit(RAW_BUFS - 1)
        for s in range(UNITS):
            gate_functions(s - LAG - 1)
            quant_rest(s - 1)
            small_quant(s - 1)
            cell_work(s - LAG - 1)
            unit_transposes(s)
            small_bank(s)
            cell_work_late(s - LAG - 1)
            load_unit(s + RAW_BUFS)
            if UNITS - 4 > s >= UNITS - 8:
                i = s - (UNITS - 8)
                nc.sync.dma_start(
                    out=wmraw[:, i * 1024 : (i + 1) * 1024], in_=Wm[i * P : (i + 1) * P, :]
                )
            gate_passes(s - LAG)
            if (s - LAG) % 4 == 0 and s - LAG >= 4:
                skip_passes((s - LAG) // 4 - 1)

        wm_banks = [wm_bank(b) for b in range(2)]
        quant_rest(UNITS - 1)
        gate_functions(UNITS - 2)
        last_th(0)
        last_ig(1)
        last_fc(1)
        last_cn(1)
        for b in range(2):
            wm_copy(b, wm_banks[b])
        wm_quant(0)
        o_banks = []
        for e in range(2):
            ob = tpp.tile([P, B], F32, tag="tp", name="ob")
            gate_group(ob[:], 15, e)
            o_banks.append(ob)
        skip_passes(3)
        wm_banks += [wm_bank(b) for b in range(2, 4)]
        ga, t = gacts[3], cell[3]
        gate_function(15, 0, o_banks[0][:])
        last_th(1)
        gate_function(15, 1, o_banks[1][:])
        for b in range(2, 4):
            wm_copy(b, wm_banks[b])
        outs = [(2 * g + u, bt) for g in range(2) for bt in range(2) for u in range(2)]
        banks = [out_transposes(jj, bt) for jj, bt in outs[0:3]]
        for e in range(2):
            nc.vector.tensor_tensor(
                out=t["y"][:, e, :], in0=ga[:, 3, e, :], in1=t["th"][:, e, :], op=ALU.mult
            )
        for e in range(2):
            skip_sum(3, e)
        mid_regroup(3)
        wm_quant(1)
        quant_mid(1)
        more = [out_transposes(jj, bt) for jj, bt in outs[3:5]]
        mps = []
        for bt in range(2):
            mp = gtp.tile([P, 512], F32, tag="gt", name="mp")
            mx(mp[:], mcod, mscl, bt * P, wmcod, wmscl, 0, 512, True, False)
            mps.append(mp)
        for item in banks + more[:1]:
            out_store(item, False)
        nc.scalar.activation(out=tiny_out[:], in_=tiny_in[:], func=AF.Exp)
        for bt in range(2):
            mx(mps[bt][:], mcod, mscl, B + bt * P, wmcod, wmscl, 512, 512, False, True)
        out_store(more[1], True)
        banks = [out_transposes(jj, bt) for jj, bt in outs[5:8]]
        ssum = const.tile([P, 2], F32)
        lsum = const.tile([P, 2], F32)
        ex = const.tile([P, 512], F32, align_bytes=256)
        mots = []
        nmxs = []
        for bt in range(2):
            mot = const.tile([P, 512], F32, name="mot%d" % bt)
            nc.vector.tensor_tensor(out=mot[:], in0=mps[bt][:], in1=bmbc[:], op=ALU.add)
            mots.append(mot)
        for bt in range(2):
            nmx = const.tile([P, 1], F32, name="nmx%d" % bt)
            nc.vector.tensor_reduce(
                out=nmx[:], in_=mots[bt][:], axis=AX.X, op=ALU.max, negate=True
            )
            nc.scalar.activation(
                out=ex[:], in_=mots[bt][:], func=AF.Exp, bias=nmx[:, 0:1], scale=1.0,
                accum_out=ssum[:, bt : bt + 1],
            )
            nmxs.append(nmx)
        nc.scalar.activation(out=lsum[:], in_=ssum[:], func=AF.Ln)
        for item in banks:
            out_store(item, True)
        for bt in range(2):
            nc.vector.tensor_scalar(
                out=mots[bt][:], in0=mots[bt][:], scalar1=nmxs[bt][:, 0:1],
                scalar2=lsum[:, bt : bt + 1], op0=ALU.add, op1=ALU.subtract,
            )
            nc.sync.dma_start(out=out_0[bt * P : (bt + 1) * P, :], in_=mots[bt][:])
